import numpy as np
import ml_dtypes


def mxq(x, axis, fmt="e4m3"):
    dtype, down = {"e4m3": (ml_dtypes.float8_e4m3fn, 7), "e5m2": (ml_dtypes.float8_e5m2, 14)}[fmt]
    v = np.moveaxis(np.asarray(x, np.float32).astype(ml_dtypes.bfloat16).astype(np.float64), axis, -1)
    blocks = v.reshape(v.shape[:-1] + (-1, 32))
    amax = np.abs(blocks).max(-1, keepdims=True)
    byte = np.maximum(np.where(amax > 0, np.frexp(amax)[1] - 1 + 127, 0) - down, 1)
    scale = np.exp2(byte - 127.0)
    codes = (blocks / scale).astype(np.float32).astype(dtype).astype(np.float64)
    return np.moveaxis((codes * scale).reshape(v.shape), -1, axis)


WIDE = False


def mx_kscale(k):
    if not WIDE:
        return np.ones(k)
    levels = np.array([10, -10, 5, -5, 0])
    a = np.random.permutation(np.resize(levels, k // 512 * 4)).reshape(k // 512, 4)
    idx = np.arange(k)
    return np.exp2(a[idx // 512, idx % 128 // 32])


BF16 = ml_dtypes.bfloat16


def bf(x):
    return np.asarray(x, np.float32).astype(BF16)


def f64(x):
    return np.asarray(x).astype(np.float64)


B, S, H, D = 2, 512, 16, 64
E = H * D
HALF = D // 2


def rotate_half(u):
    u1, u2 = np.split(u, 2, axis=-1)
    return np.concatenate([-u2, u1], axis=-1)


def apply_rope(t, sin, cos):
    x1, x2 = np.split(t, 2, axis=-1)
    x_rot = x1 * cos + rotate_half(x1) * sin
    return np.concatenate([x_rot, x2], axis=-1)


def setup_inputs():
    s = mx_kscale(E)
    th = np.random.uniform(0.0, 2.0 * np.pi, (S, HALF))
    return {"x": bf(np.random.standard_normal((B, S, E)) * s),
            "W_qkv": bf(np.random.standard_normal((E, 3 * E)) / np.sqrt(E) / s[:, None]),
            "b_qkv": bf(np.random.standard_normal(3 * E) * 0.2),
            "sin_tab": bf(np.sin(th)),
            "cos_tab": bf(np.cos(th))}


def reference(x, W_qkv, b_qkv, sin_tab, cos_tab):
    qkv = (mxq(f64(x), 2, "e4m3") @ mxq(f64(W_qkv), 0, "e4m3")) + f64(b_qkv)
    q, k, v = np.split(qkv, 3, axis=-1)
    q = q.reshape(B, S, H, D)
    k = k.reshape(B, S, H, D)
    v = v.reshape(B, S, H, D)
    sin = f64(sin_tab)[None, :, None, :]
    cos = f64(cos_tab)[None, :, None, :]
    q_rot = apply_rope(q, sin, cos)
    k_rot = apply_rope(k, sin, cos)
    return q_rot, k_rot, v

@@ -1,0 +1,162 @@
+from contextlib import ExitStack
+
+import concourse.mybir as mybir
+from concourse.masks import make_identity
+
+F32 = mybir.dt.float32
+BF16 = mybir.dt.bfloat16
+U32 = mybir.dt.uint32
+U8 = mybir.dt.uint8
+FP8X4 = mybir.dt.float8_e4m3fn_x4
+ALU = mybir.AluOpType
+
+P = 128
+B, S, H, D = 2, 512, 16, 64
+E = H * D
+NPT = S // P
+CH = 512
+HPC = CH // D
+FLOPS = 2 * B * S * E * 3 * E
+
+GP_PAIRS = (1, 3)
+
+
+def tile_improvedattention_pa_kernel(tc, x, W_qkv, b_qkv, sin_tab, cos_tab, out_0, out_1, out_2):
+    nc = tc.nc
+    outs = (out_0, out_1, out_2)
+    chunks = [(0, 0), (1, 0), (2, 0), (0, 1), (1, 1), (2, 1)]
+    with ExitStack() as ctx:
+        const = ctx.enter_context(tc.tile_pool(name="const", bufs=1))
+        xin = ctx.enter_context(tc.tile_pool(name="xin", bufs=1))
+        xgp = ctx.enter_context(tc.tile_pool(name="xgp", bufs=2))
+        wrp = ctx.enter_context(tc.tile_pool(name="wrp", bufs=1))
+        wgp = ctx.enter_context(tc.tile_pool(name="wgp", bufs=2))
+        wcp = ctx.enter_context(tc.tile_pool(name="wcp", bufs=1))
+        op = ctx.enter_context(tc.tile_pool(name="op", bufs=6))
+        tp = ctx.enter_context(tc.tile_pool(name="tp", bufs=2))
+        psum = ctx.enter_context(tc.psum_pool(name="psum", bufs=8))
+
+        xp = []
+        for j in range(NPT):
+            xp.append(xin.tile([P, B, E], BF16, name="xp%d" % j))
+        wr = []
+        for c in range(len(chunks)):
+            wr.append(wrp.tile([P, 8, CH], BF16, name="wr%d" % c))
+
+        def load_x(j):
+            nc.sync.dma_start(out=xp[j][:], in_=x[:, j * P:(j + 1) * P, :].rearrange("b p k -> p b k"))
+
+        def load_w(c):
+            which, half = chunks[c]
+            c0 = which * E + half * CH
+            for gu in range(4):
+                nc.sync.dma_start(
+                    out=wr[c][:, 2 * gu:2 * gu + 2, :],
+                    in_=W_qkv[256 * gu:256 * gu + 256, c0:c0 + CH].rearrange("(q e) c -> q e c", e=2),
+                )
+
+        bias = const.tile([P, 3 * E], BF16)
+        cos16 = const.tile([P, NPT, 32], BF16)
+        sin16 = const.tile([P, NPT, 32], BF16)
+
+        load_x(0)
+        load_w(0)
+        nc.sync.dma_start(out=cos16[:], in_=cos_tab.rearrange("(t p) j -> p t j", p=P))
+        nc.sync.dma_start(out=sin16[:], in_=sin_tab.rearrange("(t p) j -> p t j", p=P))
+        nc.sync.dma_start(out=bias[:], in_=b_qkv.partition_broadcast(P))
+        for j in range(1, NPT):
+            load_x(j)
+        for c in range(1, len(chunks)):
+            load_w(c)
+
+        ident = const.tile([P, P], F32)
+        make_identity(nc, ident[:])
+
+        cs = const.tile([P, NPT, 2, 32], F32)
+        nc.vector.tensor_copy(out=cs[:, :, 0, :], in_=cos16[:])
+        nc.vector.tensor_copy(out=cs[:, :, 1, 0:16], in_=sin16[:, :, 16:32])
+        nc.vector.tensor_scalar_mul(out=cs[:, :, 1, 16:32], in0=sin16[:, :, 0:16], scalar1=-1.0)
+
+        xc = const.tile([P, NPT, B, 2, P], U32, align_bytes=64)
+        xs = const.tile([P, NPT, B, 2, P], U8, align_bytes=64)
+        for j in range(NPT):
+            xg = xgp.tile([P, B, 2, P, 4], BF16, align_bytes=64)
+            xg32 = xg[:].bitcast(F32)
+            for b in range(B):
+                xt = psum.tile([P, 4, P], F32, tag="bank")
+                xw = xp[j][:, b, :].bitcast(F32)
+                for gu in range(4):
+                    nc.tensor.transpose(xt[:, gu, :], xw[:, gu * P:(gu + 1) * P], ident[:])
+                nc.vector.tensor_copy(out=xg32[:, b], in_=xt[:].rearrange("p (g u) r -> p g r u", u=2))
+            nc.vector.quantize_mx(
+                out=xc[:, j].rearrange("p b g r -> p (b g r)").bitcast(FP8X4),
+                scales=xs[:, j].rearrange("p b g r -> p (b g r)"),
+                in_=xg[:].rearrange("p b g r t -> p (b g r t)"),
+            )
+
+        wc = []
+        ws = []
+        for c in range(len(chunks)):
+            wc.append(wcp.tile([P, 2, CH], U32, name="wc%d" % c, align_bytes=64))
+            ws.append(wcp.tile([P, 2, CH], U8, name="ws%d" % c, align_bytes=64))
+        wgs = {}
+
+        def regroup(c):
+            wg = wgp.tile([P, 2, CH, 4], BF16, align_bytes=64)
+            wgs[c] = wg
+            for g in range(2):
+                nc.scalar.copy(
+                    out=wg[:, g].rearrange("p (c i) t -> p c t i", i=4),
+                    in_=wr[c][:, 4 * g:4 * g + 4, :].rearrange("p t (c i) -> p c t i", i=4),
+                )
+
+        def quantise(c):
+            wg = wgs[c]
+            for g in range(2):
+                nc.vector.quantize_mx(
+                    out=wc[c][:, g, :].bitcast(FP8X4),
+                    scales=ws[c][:, g, :],
+                    in_=wg[:, g].rearrange("p c t -> p (c t)"),
+                )
+
+        def rope(eng, o, j):
+            t = tp.tile([P, B * HPC, 2, 32], F32, tag="t_g" if eng is nc.gpsimd else "t_v")
+            ov = o[:].rearrange("p b (h d) -> p (b h) d", d=D)
+            shape = [P, B * HPC, 2, 32]
+            eng.tensor_tensor(
+                out=t[:],
+                in0=ov[:, :, 0:32].unsqueeze(2).to_broadcast(shape),
+                in1=cs[:, j].unsqueeze(1).to_broadcast(shape),
+                op=ALU.mult,
+            )
+            eng.tensor_tensor(out=ov[:, :, 0:16], in0=t[:, :, 0, 0:16], in1=t[:, :, 1, 16:32], op=ALU.add)
+            eng.tensor_tensor(out=ov[:, :, 16:32], in0=t[:, :, 0, 16:32], in1=t[:, :, 1, 0:16], op=ALU.add)
+
+        regroup(0)
+        quantise(0)
+        for c in range(len(chunks)):
+            which, half = chunks[c]
+            c0 = which * E + half * CH
+            if c + 1 < len(chunks):
+                regroup(c + 1)
+            dst = outs[which].rearrange("b s h d -> s b (h d)")
+            for j in range(NPT):
+                o = op.tile([P, B, CH], F32)
+                for b in range(B):
+                    acc = psum.tile([P, CH], F32, tag="bank")
+                    for g in range(2):
+                        nc.tensor.matmul_mx(
+                            out=acc[:],
+                            lhsT=xc[:, j, b, g, :].bitcast(FP8X4),
+                            lhsT_scale=xs[:, j, b, g, :],
+                            rhs=wc[c][:, g, :].bitcast(FP8X4),
+                            rhs_scale=ws[c][:, g, :],
+                            start=(g == 0),
+                            stop=(g == 1),
+                        )
+                    nc.vector.tensor_tensor(out=o[:, b, :], in0=acc[:], in1=bias[:, c0:c0 + CH], op=ALU.add)
+                if which < 2:
+                    rope(nc.gpsimd if j in GP_PAIRS else nc.vector, o, j)
+                nc.sync.dma_start(out=dst[j * P:(j + 1) * P, :, half * CH:(half + 1) * CH], in_=o[:])
+                if j == 1 and c + 1 < len(chunks):
+                    quantise(c + 1)

@@ -13,73 +13,92 @@ ALU = mybir.AluOpType
 P = 128
 B, S, H, D = 2, 512, 16, 64
 E = H * D
+R = D // 2
 NPT = S // P
-CH = 512
-HPC = CH // D
+BK = 512
+HPB = BK // D
 FLOPS = 2 * B * S * E * 3 * E
 
-GP_PAIRS = (1, 3)
+CHUNKS = ((0, 0), (2, 0), (0, 1), (1, 0), (2, 1), (1, 1))
+TURNED = (0, 2, 3, 5)
+PLAIN = (1, 4)
 
 
 def tile_improvedattention_pa_kernel(tc, x, W_qkv, b_qkv, sin_tab, cos_tab, out_0, out_1, out_2):
     nc = tc.nc
     outs = (out_0, out_1, out_2)
-    chunks = [(0, 0), (1, 0), (2, 0), (0, 1), (1, 1), (2, 1)]
+    nch = len(CHUNKS)
     with ExitStack() as ctx:
         const = ctx.enter_context(tc.tile_pool(name="const", bufs=1))
         xin = ctx.enter_context(tc.tile_pool(name="xin", bufs=1))
         xgp = ctx.enter_context(tc.tile_pool(name="xgp", bufs=2))
         wrp = ctx.enter_context(tc.tile_pool(name="wrp", bufs=1))
-        wgp = ctx.enter_context(tc.tile_pool(name="wgp", bufs=2))
+        wgp = ctx.enter_context(tc.tile_pool(name="wgp", bufs=3))
         wcp = ctx.enter_context(tc.tile_pool(name="wcp", bufs=1))
-        op = ctx.enter_context(tc.tile_pool(name="op", bufs=6))
-        tp = ctx.enter_context(tc.tile_pool(name="tp", bufs=2))
+        op = ctx.enter_context(tc.tile_pool(name="op", bufs=5))
+        tp = ctx.enter_context(tc.tile_pool(name="tp", bufs=4))
         psum = ctx.enter_context(tc.psum_pool(name="psum", bufs=8))
 
         xp = []
         for j in range(NPT):
             xp.append(xin.tile([P, B, E], BF16, name="xp%d" % j))
         wr = []
-        for c in range(len(chunks)):
-            wr.append(wrp.tile([P, 8, CH], BF16, name="wr%d" % c))
+        for c in range(nch):
+            wr.append(wrp.tile([P, 8, BK], BF16, name="wr%d" % c))
 
         def load_x(j):
             nc.sync.dma_start(out=xp[j][:], in_=x[:, j * P:(j + 1) * P, :].rearrange("b p k -> p b k"))
 
         def load_w(c):
-            which, half = chunks[c]
-            c0 = which * E + half * CH
+            c0 = CHUNKS[c][0] * E + CHUNKS[c][1] * BK
             for gu in range(4):
                 nc.sync.dma_start(
                     out=wr[c][:, 2 * gu:2 * gu + 2, :],
-                    in_=W_qkv[256 * gu:256 * gu + 256, c0:c0 + CH].rearrange("(q e) c -> q e c", e=2),
+                    in_=W_qkv[256 * gu:256 * gu + 256, c0:c0 + BK].rearrange("(q e) c -> q e c", e=2),
                 )
 
         bias = const.tile([P, 3 * E], BF16)
-        cos16 = const.tile([P, NPT, 32], BF16)
-        sin16 = const.tile([P, NPT, 32], BF16)
+        cos16 = const.tile([P, NPT, R], BF16)
+        sin16 = const.tile([P, NPT, R], BF16)
+        zb = const.tile([P, P], BF16)
+        nc.vector.memset(zb[:], 0.0)
+        tab = const.tile([P, NPT, P], BF16)
+        nc.vector.memset(tab[:], 0.0)
 
-        load_x(0)
-        load_w(0)
         nc.sync.dma_start(out=cos16[:], in_=cos_tab.rearrange("(t p) j -> p t j", p=P))
         nc.sync.dma_start(out=sin16[:], in_=sin_tab.rearrange("(t p) j -> p t j", p=P))
+        b_rot = b_qkv[0:2 * E].rearrange("(r d) -> r d", d=D)[:, 0:R]
+        nc.sync.dma_start(out=zb[0:2 * H, 0:R], in_=b_rot)
+        nc.sync.dma_start(out=zb[0:2 * H, R:2 * R], in_=b_rot)
+        load_x(0)
+        load_w(0)
+        load_w(1)
         nc.sync.dma_start(out=bias[:], in_=b_qkv.partition_broadcast(P))
-        for j in range(1, NPT):
-            load_x(j)
-        for c in range(1, len(chunks)):
+        load_x(1)
+        load_x(2)
+        load_x(3)
+        for c in range(2, nch):
             load_w(c)
 
         ident = const.tile([P, P], F32)
         make_identity(nc, ident[:])
+        ident16 = const.tile([P, P], BF16)
+        nc.vector.tensor_copy(out=ident16[:], in_=ident[:])
 
-        cs = const.tile([P, NPT, 2, 32], F32)
+        cs = const.tile([P, NPT, 2, R], F32)
         nc.vector.tensor_copy(out=cs[:, :, 0, :], in_=cos16[:])
         nc.vector.tensor_copy(out=cs[:, :, 1, 0:16], in_=sin16[:, :, 16:32])
         nc.vector.tensor_scalar_mul(out=cs[:, :, 1, 16:32], in0=sin16[:, :, 0:16], scalar1=-1.0)
+        nc.vector.tensor_copy(out=tab[:, :, 0:2 * R], in_=cs[:].rearrange("p t c j -> p t (c j)"))
+        mask = const.tile([P, R], F32)
+        nc.vector.tensor_tensor(out=mask[:, 0:16], in0=ident[:, 0:16], in1=ident[:, 48:64], op=ALU.add)
+        nc.vector.tensor_tensor(out=mask[:, 16:32], in0=ident[:, 16:32], in1=ident[:, 32:48], op=ALU.add)
+
 
         xc = const.tile([P, NPT, B, 2, P], U32, align_bytes=64)
         xs = const.tile([P, NPT, B, 2, P], U8, align_bytes=64)
-        for j in range(NPT):
+
+        def x_pair(j):
             xg = xgp.tile([P, B, 2, P, 4], BF16, align_bytes=64)
             xg32 = xg[:].bitcast(F32)
             for b in range(B):
@@ -87,7 +106,7 @@ def tile_improvedattention_pa_kernel(tc, x, W_qkv, b_qkv, sin_tab, cos_tab, out_
                 xw = xp[j][:, b, :].bitcast(F32)
                 for gu in range(4):
                     nc.tensor.transpose(xt[:, gu, :], xw[:, gu * P:(gu + 1) * P], ident[:])
-                nc.vector.tensor_copy(out=xg32[:, b], in_=xt[:].rearrange("p (g u) r -> p g r u", u=2))
+                nc.scalar.copy(out=xg32[:, b], in_=xt[:].rearrange("p (g u) r -> p g r u", u=2))
             nc.vector.quantize_mx(
                 out=xc[:, j].rearrange("p b g r -> p (b g r)").bitcast(FP8X4),
                 scales=xs[:, j].rearrange("p b g r -> p (b g r)"),
@@ -96,67 +115,130 @@ def tile_improvedattention_pa_kernel(tc, x, W_qkv, b_qkv, sin_tab, cos_tab, out_
 
         wc = []
         ws = []
-        for c in range(len(chunks)):
-            wc.append(wcp.tile([P, 2, CH], U32, name="wc%d" % c, align_bytes=64))
-            ws.append(wcp.tile([P, 2, CH], U8, name="ws%d" % c, align_bytes=64))
+        for c in range(nch):
+            wc.append(wcp.tile([P, 2, BK], U32, name="wc%d" % c, align_bytes=64))
+            ws.append(wcp.tile([P, 2, BK], U8, name="ws%d" % c, align_bytes=64))
         wgs = {}
 
-        def regroup(c):
-            wg = wgp.tile([P, 2, CH, 4], BF16, align_bytes=64)
+        def regroup(c, on_vector):
+            wg = wgp.tile([P, 2, BK, 4], BF16, align_bytes=64)
             wgs[c] = wg
             for g in range(2):
-                nc.scalar.copy(
-                    out=wg[:, g].rearrange("p (c i) t -> p c t i", i=4),
-                    in_=wr[c][:, 4 * g:4 * g + 4, :].rearrange("p t (c i) -> p c t i", i=4),
-                )
+                dst = wg[:, g].rearrange("p (c i) t -> p c t i", i=4)
+                src = wr[c][:, 4 * g:4 * g + 4, :].rearrange("p t (c i) -> p c t i", i=4)
+                if on_vector:
+                    nc.vector.tensor_copy(out=dst, in_=src)
+                else:
+                    nc.scalar.copy(out=dst, in_=src)
 
         def quantise(c):
-            wg = wgs[c]
-            for g in range(2):
-                nc.vector.quantize_mx(
-                    out=wc[c][:, g, :].bitcast(FP8X4),
-                    scales=ws[c][:, g, :],
-                    in_=wg[:, g].rearrange("p c t -> p (c t)"),
-                )
-
-        def rope(eng, o, j):
-            t = tp.tile([P, B * HPC, 2, 32], F32, tag="t_g" if eng is nc.gpsimd else "t_v")
-            ov = o[:].rearrange("p b (h d) -> p (b h) d", d=D)
-            shape = [P, B * HPC, 2, 32]
-            eng.tensor_tensor(
-                out=t[:],
-                in0=ov[:, :, 0:32].unsqueeze(2).to_broadcast(shape),
-                in1=cs[:, j].unsqueeze(1).to_broadcast(shape),
-                op=ALU.mult,
+            nc.vector.quantize_mx(
+                out=wc[c][:].rearrange("p g c -> p (g c)").bitcast(FP8X4),
+                scales=ws[c][:].rearrange("p g c -> p (g c)"),
+                in_=wgs[c][:].rearrange("p g c t -> p (g c t)"),
             )
-            eng.tensor_tensor(out=ov[:, :, 0:16], in0=t[:, :, 0, 0:16], in1=t[:, :, 1, 16:32], op=ALU.add)
-            eng.tensor_tensor(out=ov[:, :, 16:32], in0=t[:, :, 0, 16:32], in1=t[:, :, 1, 0:16], op=ALU.add)
 
-        regroup(0)
-        quantise(0)
-        for c in range(len(chunks)):
-            which, half = chunks[c]
-            c0 = which * E + half * CH
-            if c + 1 < len(chunks):
-                regroup(c + 1)
+        def product(c, j, b):
+            acc = psum.tile([P, BK], F32, tag="bank")
+            for g in range(2):
+                nc.tensor.matmul_mx(
+                    out=acc[:],
+                    lhsT=xc[:, j, b, g, :].bitcast(FP8X4),
+                    lhsT_scale=xs[:, j, b, g, :],
+                    rhs=wc[c][:, g, :].bitcast(FP8X4),
+                    rhs_scale=ws[c][:, g, :],
+                    start=(g == 0),
+                    stop=(g == 1),
+                )
+            return acc
+
+        def turned_pair(c, j):
+            which, half = CHUNKS[c]
+            c0 = which * E + half * BK
+            o = op.tile([P, B, BK], F32, tag="o")
+            t = tp.tile([P, B, HPB, 2, R], F32, tag="t")
+            for b in range(B):
+                acc = product(c, j, b)
+                av = acc[:].rearrange("p (h d) -> p h d", d=D)
+                nc.vector.tensor_tensor(
+                    out=t[:, b],
+                    in0=av[:, :, 0:R].unsqueeze(2).to_broadcast([P, HPB, 2, R]),
+                    in1=cs[:, j].unsqueeze(1).to_broadcast([P, HPB, 2, R]),
+                    op=ALU.mult,
+                )
+                nc.vector.tensor_tensor(
+                    out=o[:, b, :].rearrange("p (h d) -> p h d", d=D)[:, :, R:D],
+                    in0=av[:, :, R:D],
+                    in1=bias[:, c0:c0 + BK].rearrange("p (h d) -> p h d", d=D)[:, :, R:D],
+                    op=ALU.add,
+                )
+            ov = o[:].rearrange("p b (h d) -> p (b h) d", d=D)
+            tv = t[:].rearrange("p b h c j -> p (b h) c j")
+            nc.gpsimd.tensor_tensor(out=ov[:, :, 0:16], in0=tv[:, :, 0, 0:16], in1=tv[:, :, 1, 16:32], op=ALU.add)
+            nc.gpsimd.tensor_tensor(out=ov[:, :, 16:32], in0=tv[:, :, 0, 16:32], in1=tv[:, :, 1, 0:16], op=ALU.add)
+            o4 = o[:].rearrange("p b (h d) -> p b h d", d=D)[:, :, :, 0:R]
+            r0 = which * H + half * HPB
+            nc.gpsimd.tensor_tensor(
+                out=o4,
+                in0=o4,
+                in1=brot[:, j, r0:r0 + HPB, :].unsqueeze(1).to_broadcast([P, B, HPB, R]),
+                op=ALU.add,
+            )
             dst = outs[which].rearrange("b s h d -> s b (h d)")
-            for j in range(NPT):
-                o = op.tile([P, B, CH], F32)
-                for b in range(B):
-                    acc = psum.tile([P, CH], F32, tag="bank")
-                    for g in range(2):
-                        nc.tensor.matmul_mx(
-                            out=acc[:],
-                            lhsT=xc[:, j, b, g, :].bitcast(FP8X4),
-                            lhsT_scale=xs[:, j, b, g, :],
-                            rhs=wc[c][:, g, :].bitcast(FP8X4),
-                            rhs_scale=ws[c][:, g, :],
-                            start=(g == 0),
-                            stop=(g == 1),
-                        )
-                    nc.vector.tensor_tensor(out=o[:, b, :], in0=acc[:], in1=bias[:, c0:c0 + CH], op=ALU.add)
-                if which < 2:
-                    rope(nc.gpsimd if j in GP_PAIRS else nc.vector, o, j)
-                nc.sync.dma_start(out=dst[j * P:(j + 1) * P, :, half * CH:(half + 1) * CH], in_=o[:])
-                if j == 1 and c + 1 < len(chunks):
-                    quantise(c + 1)
+            nc.sync.dma_start(out=dst[j * P:(j + 1) * P, :, half * BK:(half + 1) * BK], in_=o[:])
+
+        def plain_bank(c, j, b):
+            which, half = CHUNKS[c]
+            c0 = which * E + half * BK
+            ob = op.tile([P, BK], F32, tag="ob")
+            acc = product(c, j, b)
+            nc.vector.tensor_tensor(out=ob[:], in0=acc[:], in1=bias[:, c0:c0 + BK], op=ALU.add)
+            dst = outs[which].rearrange("b s h d -> s b (h d)")
+            nc.sync.dma_start(out=dst[j * P:(j + 1) * P, b, half * BK:(half + 1) * BK], in_=ob[:])
+
+        def turned_bias(t):
+            for w in range(2):
+                bp = psum.tile([P, BK], F32, tag="bank")
+                nc.tensor.matmul(
+                    out=bp[:],
+                    lhsT=tabT[:, t, :],
+                    rhs=bmat[:, w * H:(w + 1) * H, :].rearrange("p r j -> p (r j)"),
+                    start=True,
+                    stop=True,
+                )
+                nc.scalar.copy(out=brot[:, t, w * H:(w + 1) * H, :].rearrange("p r j -> p (r j)"), in_=bp[:])
+
+        x_pair(0)
+        regroup(0, True)
+        quantise(0)
+
+        tps = psum.tile([P, NPT, P], BF16, tag="bank")
+        for t in range(NPT):
+            nc.tensor.transpose(tps[:, t, :], tab[:, t, :], ident16[:])
+        zps = psum.tile([P, P], BF16, tag="bank")
+        nc.tensor.transpose(zps[:], zb[:], ident16[:])
+        tabT = const.tile([P, NPT, P], BF16)
+        nc.scalar.copy(out=tabT[:], in_=tps[:])
+        bmat = const.tile([P, 2 * H, R], BF16)
+        nc.vector.tensor_tensor(
+            out=bmat[:],
+            in0=zps[:, 0:2 * H].unsqueeze(2).to_broadcast([P, 2 * H, R]),
+            in1=mask[:].unsqueeze(1).to_broadcast([P, 2 * H, R]),
+            op=ALU.mult,
+        )
+        brot = const.tile([P, NPT, 2 * H, R], F32)
+
+        turned_bias(0)
+        regroup(1, False)
+        regroup_at = {1: 2, 3: 3, 5: 4, 7: 5}
+        quantise_at = {0: 1, 3: 2, 6: 3, 7: 4, 10: 5}
+        for u in range(16):
+            turned_pair(TURNED[u // NPT], u % NPT)
+            if u + 1 < NPT:
+                x_pair(u + 1)
+                turned_bias(u + 1)
+            if u in regroup_at:
+                regroup(regroup_at[u], False)
+            if u in quantise_at:
+                quantise(quantise_at[u])
+            plain_bank(PLAIN[u // 8], (u % 8) // 2, u % 2)

@@ -9,6 +9,7 @@ U32 = mybir.dt.uint32
 U8 = mybir.dt.uint8
 FP8X4 = mybir.dt.float8_e4m3fn_x4
 ALU = mybir.AluOpType
+ACT = mybir.ActivationFunctionType
 
 P = 128
 B, S, H, D = 2, 512, 16, 64
@@ -19,9 +20,44 @@ BK = 512
 HPB = BK // D
 FLOPS = 2 * B * S * E * 3 * E
 
-CHUNKS = ((0, 0), (2, 0), (0, 1), (1, 0), (2, 1), (1, 1))
-TURNED = (0, 2, 3, 5)
-PLAIN = (1, 4)
+CHUNKS = ((0,0),(0,1),(1,0),(1,1),(2,0),(2,1))
+TURNED = (0, 1, 2, 3)
+PLAIN = (4, 5)
+FROM_PSUM = (12, 13, 14, 15)
+LOADS = (("LS","cos"),("LS","sin"),("LS","zb"),("LX",0),("LW",0),("LB",0),("LX",1),("LW",4),("LX",2),("LX",3),("LW",1),("LB",1),("LW",2),("LW",3),("LW",5))
+STEPS = (
+    ("ST1",), ("TABT",), ("BMAT",), ("XT", 0, 0), ("XT", 0, 1), ("XE", 0, 0), ("RG", 0, 0), ("BP", 0),
+    ("XE", 0, 1), ("BS", 0), ("XQ", 0), ("RG", 0, 1), ("XT", 1, 0), ("WQ", 0), ("XT", 1, 1), ("XE", 1, 0),
+    ("XE", 1, 1), ("MX", 0, 0), ("RH", 4, 0, 0), ("XQ", 1), ("MX", 0, 1), ("TA", 0, 0), ("BP", 1), ("MX", 1, 0),
+    ("RH", 4, 0, 1), ("TA", 0, 1), ("XT", 2, 0), ("XT", 2, 1), ("XE", 2, 0), ("TA", 1, 0), ("G", 0), ("XT", 3, 0),
+    ("XE", 2, 1), ("XT", 3, 1), ("XE", 3, 0), ("XQ", 2), ("MX", 1, 1), ("XE", 3, 1), ("BP", 2), ("TA", 1, 1),
+    ("MX", 2, 0), ("RH", 4, 1, 0), ("MX", 2, 1), ("XQ", 3), ("BP", 3), ("RH", 4, 1, 1), ("TA", 2, 0), ("MX", 3, 0),
+    ("MX", 3, 1), ("TA", 2, 1), ("BS", 1), ("BP", 4), ("RH", 1, 0, 0), ("G", 1), ("WQ", 4), ("SO", 0),
+    ("RH", 1, 0, 1), ("TA", 3, 0), ("VP", 0), ("VP", 1), ("TA", 3, 1), ("RH", 1, 1, 0), ("VP", 2), ("SO", 1),
+    ("RG", 2, 0), ("VP", 3), ("RH", 1, 1, 1), ("VP", 4), ("RG", 2, 1), ("BS", 2), ("BS", 3), ("G", 2),
+    ("VP", 5), ("VS", 0), ("WQ", 1), ("VP", 6), ("VS", 1), ("WP", 0), ("BS", 4), ("WQ", 2),
+    ("WP", 1), ("WS", 0), ("MX", 4, 0), ("WS", 1), ("G", 3), ("MX", 4, 1), ("SO", 2), ("TA", 4, 0),
+    ("VS", 2), ("BP", 5), ("VS", 3), ("WP", 2), ("TA", 4, 1), ("BS", 5), ("WP", 3), ("WS", 2),
+    ("MX", 5, 0), ("WS", 3), ("MX", 5, 1), ("TA", 5, 0), ("RH", 5, 0, 0), ("G", 4), ("SO", 3), ("SV", 0),
+    ("BP", 6), ("MX", 6, 0), ("TA", 5, 1), ("MX", 6, 1), ("RH", 5, 0, 1), ("TA", 6, 0), ("BP", 7), ("MX", 7, 0),
+    ("RH", 5, 1, 0), ("TA", 6, 1), ("MX", 7, 1), ("G", 5), ("SO", 4), ("TA", 7, 0), ("VP", 7), ("RH", 5, 1, 1),
+    ("TA", 7, 1), ("BP", 8), ("BS", 6), ("WQ", 5), ("MX", 8, 0), ("VS", 4), ("G", 6), ("SO", 5),
+    ("BS", 7), ("WP", 4), ("VS", 5), ("TA", 8, 0), ("MX", 8, 1), ("WS", 4), ("WP", 5), ("TA", 8, 1),
+    ("BS", 8), ("VS", 6), ("VP", 8), ("WS", 5), ("WP", 6), ("G", 7), ("SO", 6), ("VS", 7),
+    ("BP", 9), ("MX", 9, 0), ("WS", 6), ("WP", 7), ("TA", 9, 0), ("BS", 9), ("MX", 9, 1), ("WS", 7),
+    ("VP", 9), ("VS", 8), ("TA", 9, 1), ("SV", 1), ("BP", 10), ("G", 8), ("RH", 3, 0, 0), ("SO", 7),
+    ("MX", 10, 0), ("WP", 8), ("TA", 10, 0), ("MX", 10, 1), ("WS", 8), ("VP", 10), ("RH", 3, 0, 1), ("TA", 10, 1),
+    ("BP", 11), ("MX", 11, 0), ("G", 9), ("SO", 8), ("RH", 3, 1, 0), ("MX", 11, 1), ("TA", 11, 0), ("VP", 11),
+    ("TA", 11, 1), ("BP", 12), ("RH", 3, 1, 1), ("VP", 12), ("VP", 13), ("BS", 10), ("WQ", 3), ("SO", 9),
+    ("VS", 9), ("G", 10), ("VP", 14), ("BS", 11), ("WP", 9), ("VS", 10), ("MX", 12, 0), ("WS", 9),
+    ("WP", 10), ("TA", 12, 0), ("VS", 11), ("MX", 12, 1), ("WS", 10), ("G", 11), ("WP", 11), ("SO", 10),
+    ("TA", 12, 1), ("VS", 12), ("BP", 13), ("MX", 13, 0), ("WS", 11), ("Y", 12), ("WP", 12), ("VS", 13),
+    ("SV", 2), ("TA", 13, 0), ("MX", 13, 1), ("WS", 12), ("WP", 13), ("VS", 14), ("TA", 13, 1), ("G", 12),
+    ("SO", 11), ("BP", 14), ("WS", 13), ("WP", 14), ("Y", 13), ("MX", 14, 0), ("WS", 14), ("G", 13),
+    ("SO", 12), ("MX", 14, 1), ("TA", 14, 0), ("VP", 15), ("TA", 14, 1), ("BP", 15), ("VS", 15), ("SO", 13),
+    ("MX", 15, 0), ("Y", 14), ("WP", 15), ("TA", 15, 0), ("G", 14), ("MX", 15, 1), ("WS", 15), ("TA", 15, 1),
+    ("SV", 3), ("SO", 14), ("Y", 15), ("G", 15), ("SO", 15),
+)
 
 
 def tile_improvedattention_pa_kernel(tc, x, W_qkv, b_qkv, sin_tab, cos_tab, out_0, out_1, out_2):
@@ -29,6 +65,7 @@ def tile_improvedattention_pa_kernel(tc, x, W_qkv, b_qkv, sin_tab, cos_tab, out_
     outs = (out_0, out_1, out_2)
     nch = len(CHUNKS)
     with ExitStack() as ctx:
+        ctx.enter_context(tc.manual_schedule())
         const = ctx.enter_context(tc.tile_pool(name="const", bufs=1))
         xin = ctx.enter_context(tc.tile_pool(name="xin", bufs=1))
         xgp = ctx.enter_context(tc.tile_pool(name="xgp", bufs=2))
@@ -37,208 +74,264 @@ def tile_improvedattention_pa_kernel(tc, x, W_qkv, b_qkv, sin_tab, cos_tab, out_
         wcp = ctx.enter_context(tc.tile_pool(name="wcp", bufs=1))
         op = ctx.enter_context(tc.tile_pool(name="op", bufs=5))
         tp = ctx.enter_context(tc.tile_pool(name="tp", bufs=4))
+        bsp = ctx.enter_context(tc.tile_pool(name="bsp", bufs=3))
+        vtp = ctx.enter_context(tc.tile_pool(name="vtp", bufs=3))
+        vop = ctx.enter_context(tc.tile_pool(name="vop", bufs=2))
         psum = ctx.enter_context(tc.psum_pool(name="psum", bufs=8))
 
         xp = []
         for j in range(NPT):
             xp.append(xin.tile([P, B, E], BF16, name="xp%d" % j))
         wr = []
+        wc = []
+        ws = []
         for c in range(nch):
             wr.append(wrp.tile([P, 8, BK], BF16, name="wr%d" % c))
-
-        def load_x(j):
-            nc.sync.dma_start(out=xp[j][:], in_=x[:, j * P:(j + 1) * P, :].rearrange("b p k -> p b k"))
-
-        def load_w(c):
-            c0 = CHUNKS[c][0] * E + CHUNKS[c][1] * BK
-            for gu in range(4):
-                nc.sync.dma_start(
-                    out=wr[c][:, 2 * gu:2 * gu + 2, :],
-                    in_=W_qkv[256 * gu:256 * gu + 256, c0:c0 + BK].rearrange("(q e) c -> q e c", e=2),
-                )
-
-        bias = const.tile([P, 3 * E], BF16)
+            wc.append(wcp.tile([P, 2, BK], U32, name="wc%d" % c, align_bytes=64))
+            ws.append(wcp.tile([P, 2, BK], U8, name="ws%d" % c, align_bytes=64))
+        bias = const.tile([P, 2 * E], BF16)
         cos16 = const.tile([P, NPT, R], BF16)
         sin16 = const.tile([P, NPT, R], BF16)
         zb = const.tile([P, P], BF16)
-        nc.vector.memset(zb[:], 0.0)
         tab = const.tile([P, NPT, P], BF16)
-        nc.vector.memset(tab[:], 0.0)
-
-        nc.sync.dma_start(out=cos16[:], in_=cos_tab.rearrange("(t p) j -> p t j", p=P))
-        nc.sync.dma_start(out=sin16[:], in_=sin_tab.rearrange("(t p) j -> p t j", p=P))
-        b_rot = b_qkv[0:2 * E].rearrange("(r d) -> r d", d=D)[:, 0:R]
-        nc.sync.dma_start(out=zb[0:2 * H, 0:R], in_=b_rot)
-        nc.sync.dma_start(out=zb[0:2 * H, R:2 * R], in_=b_rot)
-        load_x(0)
-        load_w(0)
-        load_w(1)
-        nc.sync.dma_start(out=bias[:], in_=b_qkv.partition_broadcast(P))
-        load_x(1)
-        load_x(2)
-        load_x(3)
-        for c in range(2, nch):
-            load_w(c)
-
         ident = const.tile([P, P], F32)
-        make_identity(nc, ident[:])
         ident16 = const.tile([P, P], BF16)
-        nc.vector.tensor_copy(out=ident16[:], in_=ident[:])
-
         cs = const.tile([P, NPT, 2, R], F32)
+        mask = const.tile([P, R], F32)
+        tabT = const.tile([P, NPT, P], BF16)
+        bmat = const.tile([P, 2 * H, R], BF16)
+        bt = const.tile([P, 8], F32)
+        xc = const.tile([P, B, 2, NPT, P], U32, align_bytes=64)
+        xs = const.tile([P, B, 2, NPT, P], U8, align_bytes=64)
+
+        nc.vector.memset(zb[:], 0.0)
+        nc.vector.memset(tab[:], 0.0)
+        make_identity(nc, ident[:])
+
+        b_rot = b_qkv[0:2 * E].rearrange("(r d) -> r d", d=D)[:, 0:R]
+        for ld in LOADS:
+            if ld[0] == "LS" and ld[1] == "cos":
+                nc.sync.dma_start(out=cos16[:], in_=cos_tab.rearrange("(t p) j -> p t j", p=P))
+            elif ld[0] == "LS" and ld[1] == "sin":
+                nc.sync.dma_start(out=sin16[:], in_=sin_tab.rearrange("(t p) j -> p t j", p=P))
+            elif ld[0] == "LS":
+                nc.sync.dma_start(out=zb[0:2 * H, 0:R], in_=b_rot)
+                nc.sync.dma_start(out=zb[0:2 * H, R:2 * R], in_=b_rot)
+                nc.sync.dma_start(out=zb[2 * H:2 * H + 8, :], in_=b_qkv[2 * E:3 * E].rearrange("(r c) -> r c", c=P))
+            elif ld[0] == "LX":
+                j = ld[1]
+                nc.sync.dma_start(out=xp[j][:], in_=x[:, j * P:(j + 1) * P, :].rearrange("b p k -> p b k"))
+            elif ld[0] == "LW":
+                c = ld[1]
+                c0 = CHUNKS[c][0] * E + CHUNKS[c][1] * BK
+                for gu in range(4):
+                    nc.sync.dma_start(
+                        out=wr[c][:, 2 * gu:2 * gu + 2, :],
+                        in_=W_qkv[256 * gu:256 * gu + 256, c0:c0 + BK].rearrange("(q e) c -> q e c", e=2),
+                    )
+            else:
+                w = ld[1]
+                nc.sync.dma_start(out=bias[:, w * E:(w + 1) * E], in_=b_qkv[w * E:(w + 1) * E].partition_broadcast(P))
+
+        nc.vector.tensor_copy(out=ident16[:], in_=ident[:])
+        nc.vector.tensor_tensor(out=mask[:, 0:16], in0=ident[:, 0:16], in1=ident[:, 48:64], op=ALU.add)
+        nc.vector.tensor_tensor(out=mask[:, 16:32], in0=ident[:, 16:32], in1=ident[:, 32:48], op=ALU.add)
         nc.vector.tensor_copy(out=cs[:, :, 0, :], in_=cos16[:])
         nc.vector.tensor_copy(out=cs[:, :, 1, 0:16], in_=sin16[:, :, 16:32])
         nc.vector.tensor_scalar_mul(out=cs[:, :, 1, 16:32], in0=sin16[:, :, 0:16], scalar1=-1.0)
         nc.vector.tensor_copy(out=tab[:, :, 0:2 * R], in_=cs[:].rearrange("p t c j -> p t (c j)"))
-        mask = const.tile([P, R], F32)
-        nc.vector.tensor_tensor(out=mask[:, 0:16], in0=ident[:, 0:16], in1=ident[:, 48:64], op=ALU.add)
-        nc.vector.tensor_tensor(out=mask[:, 16:32], in0=ident[:, 16:32], in1=ident[:, 32:48], op=ALU.add)
 
-
-        xc = const.tile([P, NPT, B, 2, P], U32, align_bytes=64)
-        xs = const.tile([P, NPT, B, 2, P], U8, align_bytes=64)
-
-        def x_pair(j):
-            xg = xgp.tile([P, B, 2, P, 4], BF16, align_bytes=64)
-            xg32 = xg[:].bitcast(F32)
-            for b in range(B):
-                xt = psum.tile([P, 4, P], F32, tag="bank")
+        live = {}
+        for st in STEPS:
+            k = st[0]
+            if k == "XT":
+                j, b = st[1], st[2]
+                xt = psum.tile([P, 4, P], F32, name="xt", tag="bank")
+                live[("xt", j, b)] = xt
                 xw = xp[j][:, b, :].bitcast(F32)
                 for gu in range(4):
                     nc.tensor.transpose(xt[:, gu, :], xw[:, gu * P:(gu + 1) * P], ident[:])
-                nc.scalar.copy(out=xg32[:, b], in_=xt[:].rearrange("p (g u) r -> p g r u", u=2))
-            nc.vector.quantize_mx(
-                out=xc[:, j].rearrange("p b g r -> p (b g r)").bitcast(FP8X4),
-                scales=xs[:, j].rearrange("p b g r -> p (b g r)"),
-                in_=xg[:].rearrange("p b g r t -> p (b g r t)"),
-            )
-
-        wc = []
-        ws = []
-        for c in range(nch):
-            wc.append(wcp.tile([P, 2, BK], U32, name="wc%d" % c, align_bytes=64))
-            ws.append(wcp.tile([P, 2, BK], U8, name="ws%d" % c, align_bytes=64))
-        wgs = {}
-
-        def regroup(c, on_vector):
-            wg = wgp.tile([P, 2, BK, 4], BF16, align_bytes=64)
-            wgs[c] = wg
-            for g in range(2):
-                dst = wg[:, g].rearrange("p (c i) t -> p c t i", i=4)
-                src = wr[c][:, 4 * g:4 * g + 4, :].rearrange("p t (c i) -> p c t i", i=4)
-                if on_vector:
+            elif k == "XE":
+                j, b = st[1], st[2]
+                if ("xg", j) not in live:
+                    live[("xg", j)] = xgp.tile([P, B, 2, P, 4], BF16, name="xg", tag="xg", align_bytes=64)
+                nc.scalar.copy(
+                    out=live[("xg", j)][:].bitcast(F32)[:, b],
+                    in_=live[("xt", j, b)][:].rearrange("p (g u) r -> p g r u", u=2),
+                )
+            elif k == "XQ":
+                j = st[1]
+                for b in range(B):
+                    for g in range(2):
+                        nc.vector.quantize_mx(
+                            out=xc[:, b, g, j, :].bitcast(FP8X4),
+                            scales=xs[:, b, g, j, :],
+                            in_=live[("xg", j)][:, b, g].rearrange("p r t -> p (r t)"),
+                        )
+            elif k == "RG" or k == "RH":
+                c, g = st[1], st[2]
+                if ("wg", c) not in live:
+                    live[("wg", c)] = wgp.tile([P, 2, BK, 4], BF16, name="wg", tag="wg", align_bytes=64)
+                lo, hi = 0, BK
+                if k == "RH":
+                    lo, hi = st[3] * (BK // 2), (st[3] + 1) * (BK // 2)
+                dst = live[("wg", c)][:, g, lo:hi, :].rearrange("p (c i) t -> p c t i", i=4)
+                src = wr[c][:, 4 * g:4 * g + 4, lo:hi].rearrange("p t (c i) -> p c t i", i=4)
+                if k == "RG":
                     nc.vector.tensor_copy(out=dst, in_=src)
                 else:
                     nc.scalar.copy(out=dst, in_=src)
-
-        def quantise(c):
-            nc.vector.quantize_mx(
-                out=wc[c][:].rearrange("p g c -> p (g c)").bitcast(FP8X4),
-                scales=ws[c][:].rearrange("p g c -> p (g c)"),
-                in_=wgs[c][:].rearrange("p g c t -> p (g c t)"),
-            )
-
-        def product(c, j, b):
-            acc = psum.tile([P, BK], F32, tag="bank")
-            for g in range(2):
-                nc.tensor.matmul_mx(
-                    out=acc[:],
-                    lhsT=xc[:, j, b, g, :].bitcast(FP8X4),
-                    lhsT_scale=xs[:, j, b, g, :],
-                    rhs=wc[c][:, g, :].bitcast(FP8X4),
-                    rhs_scale=ws[c][:, g, :],
-                    start=(g == 0),
-                    stop=(g == 1),
+            elif k == "WQ":
+                c = st[1]
+                nc.vector.quantize_mx(
+                    out=wc[c][:].rearrange("p g c -> p (g c)").bitcast(FP8X4),
+                    scales=ws[c][:].rearrange("p g c -> p (g c)"),
+                    in_=live[("wg", c)][:].rearrange("p g c t -> p (g c t)"),
                 )
-            return acc
-
-        def turned_pair(c, j):
-            which, half = CHUNKS[c]
-            c0 = which * E + half * BK
-            o = op.tile([P, B, BK], F32, tag="o")
-            t = tp.tile([P, B, HPB, 2, R], F32, tag="t")
-            for b in range(B):
-                acc = product(c, j, b)
-                av = acc[:].rearrange("p (h d) -> p h d", d=D)
+            elif k == "ST1":
+                tps = psum.tile([P, NPT, P], BF16, name="tps", tag="bank")
+                for t in range(NPT):
+                    nc.tensor.transpose(tps[:, t, :], tab[:, t, :], ident16[:])
+                zps = psum.tile([P, P], BF16, name="zps", tag="bank")
+                nc.tensor.transpose(zps[:], zb[:], ident16[:])
+                live["tps"] = tps
+                live["zps"] = zps
+            elif k == "TABT":
+                nc.scalar.copy(out=tabT[:], in_=live["tps"][:])
+            elif k == "BMAT":
                 nc.vector.tensor_tensor(
-                    out=t[:, b],
-                    in0=av[:, :, 0:R].unsqueeze(2).to_broadcast([P, HPB, 2, R]),
-                    in1=cs[:, j].unsqueeze(1).to_broadcast([P, HPB, 2, R]),
+                    out=bmat[:],
+                    in0=live["zps"][:, 0:2 * H].unsqueeze(2).to_broadcast([P, 2 * H, R]),
+                    in1=mask[:].unsqueeze(1).to_broadcast([P, 2 * H, R]),
                     op=ALU.mult,
                 )
-                nc.vector.tensor_tensor(
-                    out=o[:, b, :].rearrange("p (h d) -> p h d", d=D)[:, :, R:D],
-                    in0=av[:, :, R:D],
-                    in1=bias[:, c0:c0 + BK].rearrange("p (h d) -> p h d", d=D)[:, :, R:D],
-                    op=ALU.add,
-                )
-            ov = o[:].rearrange("p b (h d) -> p (b h) d", d=D)
-            tv = t[:].rearrange("p b h c j -> p (b h) c j")
-            nc.gpsimd.tensor_tensor(out=ov[:, :, 0:16], in0=tv[:, :, 0, 0:16], in1=tv[:, :, 1, 16:32], op=ALU.add)
-            nc.gpsimd.tensor_tensor(out=ov[:, :, 16:32], in0=tv[:, :, 0, 16:32], in1=tv[:, :, 1, 0:16], op=ALU.add)
-            o4 = o[:].rearrange("p b (h d) -> p b h d", d=D)[:, :, :, 0:R]
-            r0 = which * H + half * HPB
-            nc.gpsimd.tensor_tensor(
-                out=o4,
-                in0=o4,
-                in1=brot[:, j, r0:r0 + HPB, :].unsqueeze(1).to_broadcast([P, B, HPB, R]),
-                op=ALU.add,
-            )
-            dst = outs[which].rearrange("b s h d -> s b (h d)")
-            nc.sync.dma_start(out=dst[j * P:(j + 1) * P, :, half * BK:(half + 1) * BK], in_=o[:])
-
-        def plain_bank(c, j, b):
-            which, half = CHUNKS[c]
-            c0 = which * E + half * BK
-            ob = op.tile([P, BK], F32, tag="ob")
-            acc = product(c, j, b)
-            nc.vector.tensor_tensor(out=ob[:], in0=acc[:], in1=bias[:, c0:c0 + BK], op=ALU.add)
-            dst = outs[which].rearrange("b s h d -> s b (h d)")
-            nc.sync.dma_start(out=dst[j * P:(j + 1) * P, b, half * BK:(half + 1) * BK], in_=ob[:])
-
-        def turned_bias(t):
-            for w in range(2):
-                bp = psum.tile([P, BK], F32, tag="bank")
-                nc.tensor.matmul(
-                    out=bp[:],
-                    lhsT=tabT[:, t, :],
-                    rhs=bmat[:, w * H:(w + 1) * H, :].rearrange("p r j -> p (r j)"),
-                    start=True,
-                    stop=True,
-                )
-                nc.scalar.copy(out=brot[:, t, w * H:(w + 1) * H, :].rearrange("p r j -> p (r j)"), in_=bp[:])
-
-        x_pair(0)
-        regroup(0, True)
-        quantise(0)
-
-        tps = psum.tile([P, NPT, P], BF16, tag="bank")
-        for t in range(NPT):
-            nc.tensor.transpose(tps[:, t, :], tab[:, t, :], ident16[:])
-        zps = psum.tile([P, P], BF16, tag="bank")
-        nc.tensor.transpose(zps[:], zb[:], ident16[:])
-        tabT = const.tile([P, NPT, P], BF16)
-        nc.scalar.copy(out=tabT[:], in_=tps[:])
-        bmat = const.tile([P, 2 * H, R], BF16)
-        nc.vector.tensor_tensor(
-            out=bmat[:],
-            in0=zps[:, 0:2 * H].unsqueeze(2).to_broadcast([P, 2 * H, R]),
-            in1=mask[:].unsqueeze(1).to_broadcast([P, 2 * H, R]),
-            op=ALU.mult,
-        )
-        brot = const.tile([P, NPT, 2 * H, R], F32)
-
-        turned_bias(0)
-        regroup(1, False)
-        regroup_at = {1: 2, 3: 3, 5: 4, 7: 5}
-        quantise_at = {0: 1, 3: 2, 6: 3, 7: 4, 10: 5}
-        for u in range(16):
-            turned_pair(TURNED[u // NPT], u % NPT)
-            if u + 1 < NPT:
-                x_pair(u + 1)
-                turned_bias(u + 1)
-            if u in regroup_at:
-                regroup(regroup_at[u], False)
-            if u in quantise_at:
-                quantise(quantise_at[u])
-            plain_bank(PLAIN[u // 8], (u % 8) // 2, u % 2)
+                nc.vector.tensor_copy(out=bt[:], in_=live["zps"][:, 2 * H:2 * H + 8])
+            elif k in ("BP", "BS", "MX", "TA", "Y", "G", "SO"):
+                u = st[1]
+                c = TURNED[u // NPT]
+                j = u % NPT
+                which, half = CHUNKS[c]
+                c0 = which * E + half * BK
+                r0 = which * H + half * HPB
+                if k == "BP":
+                    bp = psum.tile([P, HPB, R], F32, name="bp", tag="bank")
+                    live[("bp", u)] = bp
+                    nc.tensor.matmul(
+                        out=bp[:].rearrange("p h j -> p (h j)"),
+                        lhsT=tabT[:, j, :],
+                        rhs=bmat[:, r0:r0 + HPB, :].rearrange("p r j -> p (r j)"),
+                        start=True,
+                        stop=True,
+                    )
+                elif k == "BS":
+                    live[("bs", u)] = bsp.tile([P, HPB, R], F32, name="bs", tag="bs")
+                    nc.scalar.copy(out=live[("bs", u)][:], in_=live[("bp", u)][:])
+                elif k == "MX":
+                    b = st[2]
+                    acc = psum.tile([P, BK], F32, name="acc", tag="bank")
+                    live[("acc", u, b)] = acc
+                    for g in range(2):
+                        nc.tensor.matmul_mx(
+                            out=acc[:],
+                            lhsT=xc[:, b, g, j, :].bitcast(FP8X4),
+                            lhsT_scale=xs[:, b, g, j, :],
+                            rhs=wc[c][:, g, :].bitcast(FP8X4),
+                            rhs_scale=ws[c][:, g, :],
+                            start=(g == 0),
+                            stop=(g == 1),
+                        )
+                elif k == "TA":
+                    b = st[2]
+                    if ("t", u) not in live:
+                        live[("t", u)] = tp.tile([P, B, HPB, 2, R], F32, name="t", tag="t")
+                        live[("o", u)] = op.tile([P, B, BK], F32, name="o", tag="o")
+                    av = live[("acc", u, b)][:].rearrange("p (h d) -> p h d", d=D)
+                    nc.vector.tensor_tensor(
+                        out=live[("t", u)][:, b],
+                        in0=av[:, :, 0:R].unsqueeze(2).to_broadcast([P, HPB, 2, R]),
+                        in1=cs[:, j].unsqueeze(1).to_broadcast([P, HPB, 2, R]),
+                        op=ALU.mult,
+                    )
+                    nc.vector.tensor_tensor(
+                        out=live[("o", u)][:, b, :].rearrange("p (h d) -> p h d", d=D)[:, :, R:D],
+                        in0=av[:, :, R:D],
+                        in1=bias[:, c0:c0 + BK].rearrange("p (h d) -> p h d", d=D)[:, :, R:D],
+                        op=ALU.add,
+                    )
+                elif k == "Y":
+                    tc0 = live[("t", u)][:, :, :, 0, :]
+                    nc.vector.tensor_tensor(
+                        out=tc0,
+                        in0=tc0,
+                        in1=live[("bp", u)][:].unsqueeze(1).to_broadcast([P, B, HPB, R]),
+                        op=ALU.add,
+                    )
+                elif k == "G":
+                    o = live[("o", u)]
+                    ov = o[:].rearrange("p b (h d) -> p (b h) d", d=D)
+                    tv = live[("t", u)][:].rearrange("p b h c j -> p (b h) c j")
+                    nc.gpsimd.tensor_tensor(
+                        out=ov[:, :, 0:16], in0=tv[:, :, 0, 0:16], in1=tv[:, :, 1, 16:32], op=ALU.add
+                    )
+                    nc.gpsimd.tensor_tensor(
+                        out=ov[:, :, 16:32], in0=tv[:, :, 0, 16:32], in1=tv[:, :, 1, 0:16], op=ALU.add
+                    )
+                    if u not in FROM_PSUM:
+                        o4 = o[:].rearrange("p b (h d) -> p b h d", d=D)[:, :, :, 0:R]
+                        nc.gpsimd.tensor_tensor(
+                            out=o4,
+                            in0=o4,
+                            in1=live[("bs", u)][:].unsqueeze(1).to_broadcast([P, B, HPB, R]),
+                            op=ALU.add,
+                        )
+                else:
+                    dst = outs[which].rearrange("b s h d -> s b (h d)")
+                    nc.sync.dma_start(
+                        out=dst[j * P:(j + 1) * P, :, half * BK:(half + 1) * BK], in_=live[("o", u)][:]
+                    )
+            else:
+                n = st[1]
+                if k == "SV":
+                    c = PLAIN[n // 2]
+                    b = n % 2
+                    half = CHUNKS[c][1]
+                    dst = out_2.rearrange("b (j p) h d -> p b j (h d)", p=P)
+                    nc.sync.dma_start(out=dst[:, b, :, half * BK:(half + 1) * BK], in_=live[("ovt", n)][:])
+                else:
+                    c = PLAIN[n // 8]
+                    b = (n // 4) % 2
+                    ft = n % 4
+                    half = CHUNKS[c][1]
+                    if k == "VP":
+                        acct = psum.tile([P, BK], F32, name="acct", tag="bank")
+                        live[("at", n)] = acct
+                        for g in range(2):
+                            nc.tensor.matmul_mx(
+                                out=acct[:],
+                                lhsT=wc[c][:, g, ft * P:(ft + 1) * P].bitcast(FP8X4),
+                                lhsT_scale=ws[c][:, g, ft * P:(ft + 1) * P],
+                                rhs=xc[:, b, g].rearrange("p j r -> p (j r)").bitcast(FP8X4),
+                                rhs_scale=xs[:, b, g].rearrange("p j r -> p (j r)"),
+                                start=(g == 0),
+                                stop=(g == 1),
+                            )
+                    elif k == "VS":
+                        live[("vt", n)] = vtp.tile([P, BK], F32, name="vt", tag="vt")
+                        nc.scalar.activation(
+                            out=live[("vt", n)][:],
+                            in_=live[("at", n)][:],
+                            func=ACT.Identity,
+                            bias=bt[:, half * 4 + ft:half * 4 + ft + 1],
+                            scale=1.0,
+                        )
+                    elif k == "WP":
+                        tb = psum.tile([P, NPT, P], F32, name="tb", tag="bank")
+                        live[("tb", n)] = tb
+                        for j in range(NPT):
+                            nc.tensor.transpose(tb[:, j, :], live[("vt", n)][:, j * P:(j + 1) * P], ident[:])
+                    else:
+                        if ("ovt", n // 4) not in live:
+                            live[("ovt", n // 4)] = vop.tile([P, NPT, BK], F32, name="ovt", tag="ovt")
+                        nc.scalar.copy(
+                            out=live[("ovt", n // 4)][:, :, ft * P:(ft + 1) * P], in_=live[("tb", n)][:]
+                        )

@@ -23,40 +23,41 @@ FLOPS = 2 * B * S * E * 3 * E
 CHUNKS = ((0,0),(0,1),(1,0),(1,1),(2,0),(2,1))
 TURNED = (0, 1, 2, 3)
 PLAIN = (4, 5)
-FROM_PSUM = (12, 13, 14, 15)
-LOADS = (("LS","cos"),("LS","sin"),("LS","zb"),("LX",0),("LW",0),("LB",0),("LX",1),("LW",4),("LX",2),("LX",3),("LW",1),("LB",1),("LW",2),("LW",3),("LW",5))
+FROM_PSUM = (2, 3, 4, 5, 6, 7, 8, 9, 10, 11, 12, 13, 14, 15)
+LOADS = (("LS","cos"),("LS","sin"),("LS","zb"),("LX",0),("LW",0),("LX",1),("LW",4),("LX",2),("LX",3),("LW",1),("LW",2),("LW",3),("LW",5))
 STEPS = (
-    ("ST1",), ("TABT",), ("BMAT",), ("XT", 0, 0), ("XT", 0, 1), ("XE", 0, 0), ("RG", 0, 0), ("BP", 0),
-    ("XE", 0, 1), ("BS", 0), ("XQ", 0), ("RG", 0, 1), ("XT", 1, 0), ("WQ", 0), ("XT", 1, 1), ("XE", 1, 0),
-    ("XE", 1, 1), ("MX", 0, 0), ("RH", 4, 0, 0), ("XQ", 1), ("MX", 0, 1), ("TA", 0, 0), ("BP", 1), ("MX", 1, 0),
-    ("RH", 4, 0, 1), ("TA", 0, 1), ("XT", 2, 0), ("XT", 2, 1), ("XE", 2, 0), ("TA", 1, 0), ("G", 0), ("XT", 3, 0),
-    ("XE", 2, 1), ("XT", 3, 1), ("XE", 3, 0), ("XQ", 2), ("MX", 1, 1), ("XE", 3, 1), ("BP", 2), ("TA", 1, 1),
-    ("MX", 2, 0), ("RH", 4, 1, 0), ("MX", 2, 1), ("XQ", 3), ("BP", 3), ("RH", 4, 1, 1), ("TA", 2, 0), ("MX", 3, 0),
-    ("MX", 3, 1), ("TA", 2, 1), ("BS", 1), ("BP", 4), ("RH", 1, 0, 0), ("G", 1), ("WQ", 4), ("SO", 0),
-    ("RH", 1, 0, 1), ("TA", 3, 0), ("VP", 0), ("VP", 1), ("TA", 3, 1), ("RH", 1, 1, 0), ("VP", 2), ("SO", 1),
-    ("RG", 2, 0), ("VP", 3), ("RH", 1, 1, 1), ("VP", 4), ("RG", 2, 1), ("BS", 2), ("BS", 3), ("G", 2),
-    ("VP", 5), ("VS", 0), ("WQ", 1), ("VP", 6), ("VS", 1), ("WP", 0), ("BS", 4), ("WQ", 2),
-    ("WP", 1), ("WS", 0), ("MX", 4, 0), ("WS", 1), ("G", 3), ("MX", 4, 1), ("SO", 2), ("TA", 4, 0),
-    ("VS", 2), ("BP", 5), ("VS", 3), ("WP", 2), ("TA", 4, 1), ("BS", 5), ("WP", 3), ("WS", 2),
-    ("MX", 5, 0), ("WS", 3), ("MX", 5, 1), ("TA", 5, 0), ("RH", 5, 0, 0), ("G", 4), ("SO", 3), ("SV", 0),
-    ("BP", 6), ("MX", 6, 0), ("TA", 5, 1), ("MX", 6, 1), ("RH", 5, 0, 1), ("TA", 6, 0), ("BP", 7), ("MX", 7, 0),
-    ("RH", 5, 1, 0), ("TA", 6, 1), ("MX", 7, 1), ("G", 5), ("SO", 4), ("TA", 7, 0), ("VP", 7), ("RH", 5, 1, 1),
-    ("TA", 7, 1), ("BP", 8), ("BS", 6), ("WQ", 5), ("MX", 8, 0), ("VS", 4), ("G", 6), ("SO", 5),
-    ("BS", 7), ("WP", 4), ("VS", 5), ("TA", 8, 0), ("MX", 8, 1), ("WS", 4), ("WP", 5), ("TA", 8, 1),
-    ("BS", 8), ("VS", 6), ("VP", 8), ("WS", 5), ("WP", 6), ("G", 7), ("SO", 6), ("VS", 7),
-    ("BP", 9), ("MX", 9, 0), ("WS", 6), ("WP", 7), ("TA", 9, 0), ("BS", 9), ("MX", 9, 1), ("WS", 7),
-    ("VP", 9), ("VS", 8), ("TA", 9, 1), ("SV", 1), ("BP", 10), ("G", 8), ("RH", 3, 0, 0), ("SO", 7),
-    ("MX", 10, 0), ("WP", 8), ("TA", 10, 0), ("MX", 10, 1), ("WS", 8), ("VP", 10), ("RH", 3, 0, 1), ("TA", 10, 1),
-    ("BP", 11), ("MX", 11, 0), ("G", 9), ("SO", 8), ("RH", 3, 1, 0), ("MX", 11, 1), ("TA", 11, 0), ("VP", 11),
-    ("TA", 11, 1), ("BP", 12), ("RH", 3, 1, 1), ("VP", 12), ("VP", 13), ("BS", 10), ("WQ", 3), ("SO", 9),
-    ("VS", 9), ("G", 10), ("VP", 14), ("BS", 11), ("WP", 9), ("VS", 10), ("MX", 12, 0), ("WS", 9),
-    ("WP", 10), ("TA", 12, 0), ("VS", 11), ("MX", 12, 1), ("WS", 10), ("G", 11), ("WP", 11), ("SO", 10),
-    ("TA", 12, 1), ("VS", 12), ("BP", 13), ("MX", 13, 0), ("WS", 11), ("Y", 12), ("WP", 12), ("VS", 13),
-    ("SV", 2), ("TA", 13, 0), ("MX", 13, 1), ("WS", 12), ("WP", 13), ("VS", 14), ("TA", 13, 1), ("G", 12),
-    ("SO", 11), ("BP", 14), ("WS", 13), ("WP", 14), ("Y", 13), ("MX", 14, 0), ("WS", 14), ("G", 13),
-    ("SO", 12), ("MX", 14, 1), ("TA", 14, 0), ("VP", 15), ("TA", 14, 1), ("BP", 15), ("VS", 15), ("SO", 13),
-    ("MX", 15, 0), ("Y", 14), ("WP", 15), ("TA", 15, 0), ("G", 14), ("MX", 15, 1), ("WS", 15), ("TA", 15, 1),
-    ("SV", 3), ("SO", 14), ("Y", 15), ("G", 15), ("SO", 15),
+    ("ST1",), ("TABT",), ("BMAT",), ("XT", 0, 0), ("XT", 0, 1), ("XE", 0, 0), ("XE", 0, 1), ("BBP", 0),
+    ("RG", 0, 0), ("BBP", 1), ("BBS", 0), ("BP", 0), ("BBS", 1), ("XQ", 0), ("BS", 0), ("RG", 0, 1),
+    ("XT", 1, 0), ("WQ", 0), ("XT", 1, 1), ("XE", 1, 0), ("XE", 1, 1), ("MX", 0, 0), ("RH", 4, 0, 0), ("XQ", 1),
+    ("MX", 0, 1), ("TA", 0, 0), ("BP", 1), ("RH", 4, 0, 1), ("MX", 1, 0), ("TA", 0, 1), ("MX", 1, 1), ("RH", 4, 1, 0),
+    ("XT", 2, 0), ("XT", 2, 1), ("TA", 1, 0), ("G", 0), ("BP", 2), ("XE", 2, 0), ("XT", 3, 0), ("XT", 3, 1),
+    ("TA", 1, 1), ("XE", 2, 1), ("XE", 3, 0), ("XE", 3, 1), ("RH", 4, 1, 1), ("XQ", 2), ("XQ", 3), ("MX", 2, 0),
+    ("BS", 1), ("RH", 1, 0, 0), ("WQ", 4), ("MX", 2, 1), ("BP", 3), ("MX", 3, 0), ("RH", 1, 0, 1), ("G", 1),
+    ("TA", 2, 0), ("VP", 0), ("VP", 1), ("TA", 2, 1), ("RH", 1, 1, 0), ("MX", 3, 1), ("SO", 0), ("VP", 2),
+    ("Y", 2), ("RH", 1, 1, 1), ("BP", 4), ("TA", 3, 0), ("VP", 3), ("G", 2), ("SO", 1), ("VS", 0),
+    ("TA", 3, 1), ("VS", 1), ("VP", 4), ("WP", 0), ("VS", 2), ("SO", 2), ("WQ", 1), ("WP", 1),
+    ("WS", 0), ("WP", 2), ("WS", 1), ("Y", 3), ("MX", 4, 0), ("WS", 2), ("G", 3), ("MX", 4, 1),
+    ("TA", 4, 0), ("VS", 3), ("BP", 5), ("RH", 2, 0, 0), ("MX", 5, 0), ("TA", 4, 1), ("WP", 3), ("SO", 3),
+    ("MX", 5, 1), ("WS", 3), ("Y", 4), ("BP", 6), ("RH", 2, 0, 1), ("MX", 6, 0), ("SV", 0), ("TA", 5, 0),
+    ("G", 4), ("MX", 6, 1), ("RH", 2, 1, 0), ("VP", 5), ("TA", 5, 1), ("BP", 7), ("SO", 4), ("RH", 2, 1, 1),
+    ("Y", 5), ("MX", 7, 0), ("TA", 6, 0), ("G", 5), ("MX", 7, 1), ("RH", 5, 0, 0), ("TA", 6, 1), ("VP", 6),
+    ("RH", 5, 0, 1), ("SO", 5), ("WQ", 2), ("VP", 7), ("RH", 5, 1, 0), ("Y", 6), ("RH", 5, 1, 1), ("TA", 7, 0),
+    ("G", 6), ("BP", 8), ("VS", 4), ("TA", 7, 1), ("MX", 8, 0), ("VS", 5), ("WP", 4), ("SO", 6),
+    ("VS", 6), ("WQ", 5), ("WP", 5), ("WS", 4), ("WP", 6), ("WS", 5), ("Y", 7), ("MX", 8, 1),
+    ("WS", 6), ("TA", 8, 0), ("G", 7), ("VP", 8), ("VS", 7), ("BP", 9), ("MX", 9, 0), ("VS", 8),
+    ("TA", 8, 1), ("WP", 7), ("RH", 3, 0, 0), ("SO", 7), ("WP", 8), ("Y", 8), ("MX", 9, 1), ("WS", 7),
+    ("TA", 9, 0), ("G", 8), ("VP", 9), ("WS", 8), ("SV", 1), ("BP", 10), ("TA", 9, 1), ("MX", 10, 0),
+    ("RH", 3, 0, 1), ("MX", 10, 1), ("SO", 8), ("Y", 9), ("VP", 10), ("RH", 3, 1, 0), ("BP", 11), ("TA", 10, 0),
+    ("G", 9), ("MX", 11, 0), ("RH", 3, 1, 1), ("MX", 11, 1), ("TA", 10, 1), ("VP", 11), ("VS", 9), ("SO", 9),
+    ("WQ", 3), ("BP", 12), ("VS", 10), ("WP", 9), ("VS", 11), ("WP", 10), ("Y", 10), ("WS", 9),
+    ("WP", 11), ("TA", 11, 0), ("WS", 10), ("G", 10), ("MX", 12, 0), ("WS", 11), ("MX", 12, 1), ("TA", 11, 1),
+    ("SV", 2), ("VP", 12), ("SO", 10), ("BP", 13), ("VS", 12), ("MX", 13, 0), ("Y", 11), ("WP", 12),
+    ("TA", 12, 0), ("G", 11), ("VP", 13), ("WS", 12), ("MX", 13, 1), ("TA", 12, 1), ("VS", 13), ("VP", 14),
+    ("SO", 11), ("Y", 12), ("WP", 13), ("VS", 14), ("BP", 14), ("TA", 13, 0), ("WS", 13), ("G", 12),
+    ("WP", 14), ("MX", 14, 0), ("WS", 14), ("TA", 13, 1), ("MX", 14, 1), ("SO", 12), ("VP", 15), ("Y", 13),
+    ("BP", 15), ("VS", 15), ("MX", 15, 0), ("TA", 14, 0), ("G", 13), ("WP", 15), ("MX", 15, 1), ("TA", 14, 1),
+    ("WS", 15), ("SO", 13), ("SV", 3), ("Y", 14), ("TA", 15, 0), ("G", 14), ("TA", 15, 1), ("SO", 14),
+    ("Y", 15), ("G", 15), ("SO", 15),
 )
 
 
@@ -89,7 +90,8 @@ def tile_improvedattention_pa_kernel(tc, x, W_qkv, b_qkv, sin_tab, cos_tab, out_
             wr.append(wrp.tile([P, 8, BK], BF16, name="wr%d" % c))
             wc.append(wcp.tile([P, 2, BK], U32, name="wc%d" % c, align_bytes=64))
             ws.append(wcp.tile([P, 2, BK], U8, name="ws%d" % c, align_bytes=64))
-        bias = const.tile([P, 2 * E], BF16)
+        sel = const.tile([P, P], BF16)
+        bias = const.tile([P, 2 * H, R], F32)
         cos16 = const.tile([P, NPT, R], BF16)
         sin16 = const.tile([P, NPT, R], BF16)
         zb = const.tile([P, P], BF16)
@@ -106,6 +108,8 @@ def tile_improvedattention_pa_kernel(tc, x, W_qkv, b_qkv, sin_tab, cos_tab, out_
 
         nc.vector.memset(zb[:], 0.0)
         nc.vector.memset(tab[:], 0.0)
+        nc.vector.memset(sel[:], 0.0)
+        nc.vector.memset(sel[64:96, :], 1.0)
         make_identity(nc, ident[:])
 
         b_rot = b_qkv[0:2 * E].rearrange("(r d) -> r d", d=D)[:, 0:R]
@@ -117,11 +121,12 @@ def tile_improvedattention_pa_kernel(tc, x, W_qkv, b_qkv, sin_tab, cos_tab, out_
             elif ld[0] == "LS":
                 nc.sync.dma_start(out=zb[0:2 * H, 0:R], in_=b_rot)
                 nc.sync.dma_start(out=zb[0:2 * H, R:2 * R], in_=b_rot)
+                nc.sync.dma_start(out=zb[0:2 * H, 2 * R:3 * R], in_=b_qkv[0:2 * E].rearrange("(r d) -> r d", d=D)[:, R:D])
                 nc.sync.dma_start(out=zb[2 * H:2 * H + 8, :], in_=b_qkv[2 * E:3 * E].rearrange("(r c) -> r c", c=P))
             elif ld[0] == "LX":
                 j = ld[1]
                 nc.sync.dma_start(out=xp[j][:], in_=x[:, j * P:(j + 1) * P, :].rearrange("b p k -> p b k"))
-            elif ld[0] == "LW":
+            else:
                 c = ld[1]
                 c0 = CHUNKS[c][0] * E + CHUNKS[c][1] * BK
                 for gu in range(4):
@@ -129,13 +134,11 @@ def tile_improvedattention_pa_kernel(tc, x, W_qkv, b_qkv, sin_tab, cos_tab, out_
                         out=wr[c][:, 2 * gu:2 * gu + 2, :],
                         in_=W_qkv[256 * gu:256 * gu + 256, c0:c0 + BK].rearrange("(q e) c -> q e c", e=2),
                     )
-            else:
-                w = ld[1]
-                nc.sync.dma_start(out=bias[:, w * E:(w + 1) * E], in_=b_qkv[w * E:(w + 1) * E].partition_broadcast(P))
 
         nc.vector.tensor_copy(out=ident16[:], in_=ident[:])
-        nc.vector.tensor_tensor(out=mask[:, 0:16], in0=ident[:, 0:16], in1=ident[:, 48:64], op=ALU.add)
-        nc.vector.tensor_tensor(out=mask[:, 16:32], in0=ident[:, 16:32], in1=ident[:, 32:48], op=ALU.add)
+        nc.vector.tensor_tensor(out=mask[:], in0=ident[:, 0:32], in1=ident[:, 64:96], op=ALU.add)
+        nc.vector.tensor_tensor(out=mask[:, 0:16], in0=mask[:, 0:16], in1=ident[:, 48:64], op=ALU.add)
+        nc.vector.tensor_tensor(out=mask[:, 16:32], in0=mask[:, 16:32], in1=ident[:, 32:48], op=ALU.add)
         nc.vector.tensor_copy(out=cs[:, :, 0, :], in_=cos16[:])
         nc.vector.tensor_copy(out=cs[:, :, 1, 0:16], in_=sin16[:, :, 16:32])
         nc.vector.tensor_scalar_mul(out=cs[:, :, 1, 16:32], in0=sin16[:, :, 0:16], scalar1=-1.0)
@@ -196,6 +199,20 @@ def tile_improvedattention_pa_kernel(tc, x, W_qkv, b_qkv, sin_tab, cos_tab, out_
                 nc.tensor.transpose(zps[:], zb[:], ident16[:])
                 live["tps"] = tps
                 live["zps"] = zps
+            elif k == "BBP":
+                w = st[1]
+                pb = psum.tile([P, H, R], F32, name="pb", tag="bank")
+                live[("pb", w)] = pb
+                nc.tensor.matmul(
+                    out=pb[:].rearrange("p h j -> p (h j)"),
+                    lhsT=sel[:],
+                    rhs=bmat[:, w * H:(w + 1) * H, :].rearrange("p r j -> p (r j)"),
+                    start=True,
+                    stop=True,
+                )
+            elif k == "BBS":
+                w = st[1]
+                nc.scalar.copy(out=bias[:, w * H:(w + 1) * H, :], in_=live[("pb", w)][:])
             elif k == "TABT":
                 nc.scalar.copy(out=tabT[:], in_=live["tps"][:])
             elif k == "BMAT":
@@ -255,7 +272,7 @@ def tile_improvedattention_pa_kernel(tc, x, W_qkv, b_qkv, sin_tab, cos_tab, out_
                     nc.vector.tensor_tensor(
                         out=live[("o", u)][:, b, :].rearrange("p (h d) -> p h d", d=D)[:, :, R:D],
                         in0=av[:, :, R:D],
-                        in1=bias[:, c0:c0 + BK].rearrange("p (h d) -> p h d", d=D)[:, :, R:D],
+                        in1=bias[:, r0:r0 + HPB, :],
                         op=ALU.add,
                     )
                 elif k == "Y":

@@ -15,340 +15,456 @@ P = 128
 B, S, H, D = 2, 512, 16, 64
 E = H * D
 R = D // 2
-NPT = S // P
-BK = 512
-HPB = BK // D
+HALF = R // 2
+TILES = S // P
+PASSES = E // (4 * P)
+BANK = 512
+HEADS = BANK // D
 FLOPS = 2 * B * S * E * 3 * E
 
-CHUNKS = ((0,0),(0,1),(1,0),(1,1),(2,0),(2,1))
-TURNED = (0, 1, 2, 3)
-PLAIN = (4, 5)
-FROM_PSUM = (2, 3, 4, 5, 6, 7, 8, 9, 10, 11, 12, 13, 14, 15)
-LOADS = (("LS","cos"),("LS","sin"),("LS","zb"),("LX",0),("LW",0),("LX",1),("LW",4),("LX",2),("LX",3),("LW",1),("LW",2),("LW",3),("LW",5))
-STEPS = (
-    ("ST1",), ("TABT",), ("BMAT",), ("XT", 0, 0), ("XT", 0, 1), ("XE", 0, 0), ("XE", 0, 1), ("BBP", 0),
-    ("RG", 0, 0), ("BBP", 1), ("BBS", 0), ("BP", 0), ("BBS", 1), ("XQ", 0), ("BS", 0), ("RG", 0, 1),
-    ("XT", 1, 0), ("WQ", 0), ("XT", 1, 1), ("XE", 1, 0), ("XE", 1, 1), ("MX", 0, 0), ("RH", 4, 0, 0), ("XQ", 1),
-    ("MX", 0, 1), ("TA", 0, 0), ("BP", 1), ("RH", 4, 0, 1), ("MX", 1, 0), ("TA", 0, 1), ("MX", 1, 1), ("RH", 4, 1, 0),
-    ("XT", 2, 0), ("XT", 2, 1), ("TA", 1, 0), ("G", 0), ("BP", 2), ("XE", 2, 0), ("XT", 3, 0), ("XT", 3, 1),
-    ("TA", 1, 1), ("XE", 2, 1), ("XE", 3, 0), ("XE", 3, 1), ("RH", 4, 1, 1), ("XQ", 2), ("XQ", 3), ("MX", 2, 0),
-    ("BS", 1), ("RH", 1, 0, 0), ("WQ", 4), ("MX", 2, 1), ("BP", 3), ("MX", 3, 0), ("RH", 1, 0, 1), ("G", 1),
-    ("TA", 2, 0), ("VP", 0), ("VP", 1), ("TA", 2, 1), ("RH", 1, 1, 0), ("MX", 3, 1), ("SO", 0), ("VP", 2),
-    ("Y", 2), ("RH", 1, 1, 1), ("BP", 4), ("TA", 3, 0), ("VP", 3), ("G", 2), ("SO", 1), ("VS", 0),
-    ("TA", 3, 1), ("VS", 1), ("VP", 4), ("WP", 0), ("VS", 2), ("SO", 2), ("WQ", 1), ("WP", 1),
-    ("WS", 0), ("WP", 2), ("WS", 1), ("Y", 3), ("MX", 4, 0), ("WS", 2), ("G", 3), ("MX", 4, 1),
-    ("TA", 4, 0), ("VS", 3), ("BP", 5), ("RH", 2, 0, 0), ("MX", 5, 0), ("TA", 4, 1), ("WP", 3), ("SO", 3),
-    ("MX", 5, 1), ("WS", 3), ("Y", 4), ("BP", 6), ("RH", 2, 0, 1), ("MX", 6, 0), ("SV", 0), ("TA", 5, 0),
-    ("G", 4), ("MX", 6, 1), ("RH", 2, 1, 0), ("VP", 5), ("TA", 5, 1), ("BP", 7), ("SO", 4), ("RH", 2, 1, 1),
-    ("Y", 5), ("MX", 7, 0), ("TA", 6, 0), ("G", 5), ("MX", 7, 1), ("RH", 5, 0, 0), ("TA", 6, 1), ("VP", 6),
-    ("RH", 5, 0, 1), ("SO", 5), ("WQ", 2), ("VP", 7), ("RH", 5, 1, 0), ("Y", 6), ("RH", 5, 1, 1), ("TA", 7, 0),
-    ("G", 6), ("BP", 8), ("VS", 4), ("TA", 7, 1), ("MX", 8, 0), ("VS", 5), ("WP", 4), ("SO", 6),
-    ("VS", 6), ("WQ", 5), ("WP", 5), ("WS", 4), ("WP", 6), ("WS", 5), ("Y", 7), ("MX", 8, 1),
-    ("WS", 6), ("TA", 8, 0), ("G", 7), ("VP", 8), ("VS", 7), ("BP", 9), ("MX", 9, 0), ("VS", 8),
-    ("TA", 8, 1), ("WP", 7), ("RH", 3, 0, 0), ("SO", 7), ("WP", 8), ("Y", 8), ("MX", 9, 1), ("WS", 7),
-    ("TA", 9, 0), ("G", 8), ("VP", 9), ("WS", 8), ("SV", 1), ("BP", 10), ("TA", 9, 1), ("MX", 10, 0),
-    ("RH", 3, 0, 1), ("MX", 10, 1), ("SO", 8), ("Y", 9), ("VP", 10), ("RH", 3, 1, 0), ("BP", 11), ("TA", 10, 0),
-    ("G", 9), ("MX", 11, 0), ("RH", 3, 1, 1), ("MX", 11, 1), ("TA", 10, 1), ("VP", 11), ("VS", 9), ("SO", 9),
-    ("WQ", 3), ("BP", 12), ("VS", 10), ("WP", 9), ("VS", 11), ("WP", 10), ("Y", 10), ("WS", 9),
-    ("WP", 11), ("TA", 11, 0), ("WS", 10), ("G", 10), ("MX", 12, 0), ("WS", 11), ("MX", 12, 1), ("TA", 11, 1),
-    ("SV", 2), ("VP", 12), ("SO", 10), ("BP", 13), ("VS", 12), ("MX", 13, 0), ("Y", 11), ("WP", 12),
-    ("TA", 12, 0), ("G", 11), ("VP", 13), ("WS", 12), ("MX", 13, 1), ("TA", 12, 1), ("VS", 13), ("VP", 14),
-    ("SO", 11), ("Y", 12), ("WP", 13), ("VS", 14), ("BP", 14), ("TA", 13, 0), ("WS", 13), ("G", 12),
-    ("WP", 14), ("MX", 14, 0), ("WS", 14), ("TA", 13, 1), ("MX", 14, 1), ("SO", 12), ("VP", 15), ("Y", 13),
-    ("BP", 15), ("VS", 15), ("MX", 15, 0), ("TA", 14, 0), ("G", 13), ("WP", 15), ("MX", 15, 1), ("TA", 14, 1),
-    ("WS", 15), ("SO", 13), ("SV", 3), ("Y", 14), ("TA", 15, 0), ("G", 14), ("TA", 15, 1), ("SO", 14),
-    ("Y", 15), ("G", 15), ("SO", 15),
-)
+CHUNKS = ((0, 0), (0, 1), (1, 0), (1, 1), (2, 0), (2, 1))
+V_CHUNKS = (4, 5)
+UNITS = 4 * TILES
+V_STEPS = 16
+V_PAIRS = V_STEPS // 2
+FEATURE_TILES = BANK // P
+VECTOR = 2
+
+
+def vector_adds_turned_bias(unit):
+    return unit % 2 == 0 or unit == UNITS - 1
+
+
+def engine_orders():
+    v_halves = []
+    for pair in range(V_PAIRS + 1):
+        if pair < V_PAIRS:
+            v_halves.append(("front", pair))
+        if pair >= 1:
+            v_halves.append(("back", pair - 1))
+
+    tensor = [("tables_T",), ("x_T", 0), ("bias_mm",), ("x_T", 1), ("unit_mm", 0), ("unit_mm", 1),
+              ("x_T", 2), ("x_T", 3), ("unit_mm", 2), ("unit_mm", 3)]
+    scalar = [("tables_out",), ("x_out", 0), ("bias_out",), ("x_out", 1), ("regroup", 4, 0), ("x_out", 2),
+              ("x_out", 3), ("regroup", 4, 1)]
+    for unit in range(4):
+        if not vector_adds_turned_bias(unit):
+            scalar.append(("turned_bias_out", unit))
+    late_regroups = [(c, g) for c in (1, 2, 5, 3) for g in range(PASSES)]
+    for c, g in late_regroups[:4]:
+        scalar.append(("regroup", c, g))
+    late_regroups = late_regroups[4:]
+    written = 0
+    for unit in range(4, UNITS + 1):
+        if unit < UNITS:
+            tensor.append(("unit_mm", unit))
+            if not vector_adds_turned_bias(unit):
+                scalar.append(("turned_bias_out", unit))
+        due = min(len(v_halves), (3 * (unit - 4) + 1) // 2)
+        while written < due:
+            half, pair = v_halves[written]
+            tensor.append(("v_mm" if half == "front" else "v_T", pair))
+            scalar.append(("v_bias" if half == "front" else "v_out", pair))
+            if late_regroups and written % 2 == 0:
+                scalar.append(("regroup",) + late_regroups[0])
+                late_regroups = late_regroups[1:]
+            written += 1
+
+    vector = [("bias_mask",), ("regroup", 0, 0), ("regroup", 0, 1), ("x_quant", 0), ("w_quant", 0), ("x_quant", 1),
+              ("unit_vec", 0), ("unit_vec", 1), ("x_quant", 2), ("x_quant", 3)]
+    quantise_after = {3: (4, 1), 6: (2,), 8: (5,), 10: (3,)}
+    for unit in range(2, UNITS):
+        vector.append(("unit_vec", unit))
+        for c in quantise_after.get(unit, ()):
+            vector.append(("w_quant", c))
+
+    gpsimd = [("unit_add", unit) for unit in range(UNITS)]
+
+    v_store_after = {7: 0, 10: 1, 12: 2, 14: 3}
+    sync = []
+    for unit in range(UNITS):
+        sync.append(("unit_store", unit))
+        if unit in v_store_after:
+            sync.append(("v_store", v_store_after[unit]))
+    return [tensor, scalar, vector, gpsimd, sync]
+
+
+def needs(step):
+    kind = step[0]
+    n = step[1] if len(step) > 1 else 0
+    if kind == "x_out":
+        return [("x_T", n)]
+    if kind == "x_quant":
+        return [("x_out", n)]
+    if kind in ("tables_out", "bias_mask"):
+        return [("tables_T",)]
+    if kind == "bias_mm":
+        return [("bias_mask",)]
+    if kind == "bias_out":
+        return [("bias_mm",)]
+    if kind == "w_quant":
+        return [("regroup", n, g) for g in range(PASSES)]
+    if kind == "unit_mm":
+        return [("tables_out",), ("bias_mask",), ("x_quant", n % TILES), ("w_quant", n // TILES)]
+    if kind == "turned_bias_out":
+        return [("unit_mm", n)]
+    if kind == "unit_vec":
+        return [("unit_mm", n), ("bias_out",)]
+    if kind == "unit_add":
+        return [("unit_vec", n)] + ([] if vector_adds_turned_bias(n) else [("turned_bias_out", n)])
+    if kind == "unit_store":
+        return [("unit_add", n)]
+    if kind == "v_mm":
+        return [("w_quant", V_CHUNKS[n // (V_PAIRS // 2)])] + [("x_quant", j) for j in range(TILES)]
+    if kind == "v_bias":
+        return [("v_mm", n), ("bias_mask",)]
+    if kind == "v_T":
+        return [("v_bias", n)]
+    if kind == "v_out":
+        return [("v_T", n)]
+    if kind == "v_store":
+        return [("v_out", 2 * n + 1)]
+    return []
+
+
+def text_order():
+    queues = engine_orders()
+    written = set()
+    order = []
+    while any(queues):
+        for q in range(len(queues)):
+            if queues[q] and all(s in written for s in needs(queues[q][0])):
+                order.append((q, queues[q][0]))
+                written.add(queues[q][0])
+                queues[q] = queues[q][1:]
+    return order
 
 
 def tile_improvedattention_pa_kernel(tc, x, W_qkv, b_qkv, sin_tab, cos_tab, out_0, out_1, out_2):
     nc = tc.nc
     outs = (out_0, out_1, out_2)
-    nch = len(CHUNKS)
     with ExitStack() as ctx:
         ctx.enter_context(tc.manual_schedule())
-        const = ctx.enter_context(tc.tile_pool(name="const", bufs=1))
-        xin = ctx.enter_context(tc.tile_pool(name="xin", bufs=1))
-        xgp = ctx.enter_context(tc.tile_pool(name="xgp", bufs=2))
-        wrp = ctx.enter_context(tc.tile_pool(name="wrp", bufs=1))
-        wgp = ctx.enter_context(tc.tile_pool(name="wgp", bufs=3))
-        wcp = ctx.enter_context(tc.tile_pool(name="wcp", bufs=1))
-        op = ctx.enter_context(tc.tile_pool(name="op", bufs=5))
-        tp = ctx.enter_context(tc.tile_pool(name="tp", bufs=4))
-        bsp = ctx.enter_context(tc.tile_pool(name="bsp", bufs=3))
-        vtp = ctx.enter_context(tc.tile_pool(name="vtp", bufs=3))
-        vop = ctx.enter_context(tc.tile_pool(name="vop", bufs=2))
+        keep = ctx.enter_context(tc.tile_pool(name="keep", bufs=1))
+        x_grouped_pool = ctx.enter_context(tc.tile_pool(name="x_grouped", bufs=2))
+        w_grouped_pool = ctx.enter_context(tc.tile_pool(name="w_grouped", bufs=3))
+        products_pool = ctx.enter_context(tc.tile_pool(name="products", bufs=4))
+        unit_out_pool = ctx.enter_context(tc.tile_pool(name="unit_out", bufs=5))
+        turned_bias_pool = ctx.enter_context(tc.tile_pool(name="turned_bias", bufs=3))
+        v_T_pool = ctx.enter_context(tc.tile_pool(name="v_T", bufs=4))
+        v_out_pool = ctx.enter_context(tc.tile_pool(name="v_out", bufs=2))
         psum = ctx.enter_context(tc.psum_pool(name="psum", bufs=8))
 
-        xp = []
-        for j in range(NPT):
-            xp.append(xin.tile([P, B, E], BF16, name="xp%d" % j))
-        wr = []
-        wc = []
-        ws = []
-        for c in range(nch):
-            wr.append(wrp.tile([P, 8, BK], BF16, name="wr%d" % c))
-            wc.append(wcp.tile([P, 2, BK], U32, name="wc%d" % c, align_bytes=64))
-            ws.append(wcp.tile([P, 2, BK], U8, name="ws%d" % c, align_bytes=64))
-        sel = const.tile([P, P], BF16)
-        bias = const.tile([P, 2 * H, R], F32)
-        cos16 = const.tile([P, NPT, R], BF16)
-        sin16 = const.tile([P, NPT, R], BF16)
-        zb = const.tile([P, P], BF16)
-        tab = const.tile([P, NPT, P], BF16)
-        ident = const.tile([P, P], F32)
-        ident16 = const.tile([P, P], BF16)
-        cs = const.tile([P, NPT, 2, R], F32)
-        mask = const.tile([P, R], F32)
-        tabT = const.tile([P, NPT, P], BF16)
-        bmat = const.tile([P, 2 * H, R], BF16)
-        bt = const.tile([P, 8], F32)
-        xc = const.tile([P, B, 2, NPT, P], U32, align_bytes=64)
-        xs = const.tile([P, B, 2, NPT, P], U8, align_bytes=64)
+        x_raw = [keep.tile([P, B, E], BF16, name="x_raw%d" % j) for j in range(TILES)]
+        w_raw = [keep.tile([P, 4 * PASSES, BANK], BF16, name="w_raw%d" % c) for c in range(len(CHUNKS))]
+        w_codes = [keep.tile([P, PASSES, BANK], U32, name="w_codes%d" % c, align_bytes=64) for c in range(len(CHUNKS))]
+        w_scales = [keep.tile([P, PASSES, BANK], U8, name="w_scales%d" % c, align_bytes=64) for c in range(len(CHUNKS))]
+        x_codes = keep.tile([P, B, PASSES, TILES, P], U32, align_bytes=64)
+        x_scales = keep.tile([P, B, PASSES, TILES, P], U8, align_bytes=64)
+        cos16 = keep.tile([P, TILES, R], BF16)
+        sin16 = keep.tile([P, TILES, R], BF16)
+        factors = keep.tile([P, TILES, 2, R], F32)
+        table = keep.tile([P, TILES, P], BF16)
+        table_T = keep.tile([P, TILES, P], BF16)
+        bias_rows = keep.tile([P, P], BF16)
+        bias_masked = keep.tile([P, 2 * H, R], BF16)
+        mask = keep.tile([P, R], F32)
+        selector = keep.tile([P, P], BF16)
+        pass_bias = keep.tile([P, 2 * H, R], F32)
+        v_bias = keep.tile([P, 2 * FEATURE_TILES], F32)
+        ident = keep.tile([P, P], F32)
+        ident16 = keep.tile([P, P], BF16)
 
-        nc.vector.memset(zb[:], 0.0)
-        nc.vector.memset(tab[:], 0.0)
-        nc.vector.memset(sel[:], 0.0)
-        nc.vector.memset(sel[64:96, :], 1.0)
+        nc.vector.memset(bias_rows[:], 0.0)
+        nc.vector.memset(table[:], 0.0)
+        nc.vector.memset(selector[:], 0.0)
+        nc.vector.memset(selector[2 * R:3 * R, :], 1.0)
         make_identity(nc, ident[:])
 
-        b_rot = b_qkv[0:2 * E].rearrange("(r d) -> r d", d=D)[:, 0:R]
-        for ld in LOADS:
-            if ld[0] == "LS" and ld[1] == "cos":
-                nc.sync.dma_start(out=cos16[:], in_=cos_tab.rearrange("(t p) j -> p t j", p=P))
-            elif ld[0] == "LS" and ld[1] == "sin":
-                nc.sync.dma_start(out=sin16[:], in_=sin_tab.rearrange("(t p) j -> p t j", p=P))
-            elif ld[0] == "LS":
-                nc.sync.dma_start(out=zb[0:2 * H, 0:R], in_=b_rot)
-                nc.sync.dma_start(out=zb[0:2 * H, R:2 * R], in_=b_rot)
-                nc.sync.dma_start(out=zb[0:2 * H, 2 * R:3 * R], in_=b_qkv[0:2 * E].rearrange("(r d) -> r d", d=D)[:, R:D])
-                nc.sync.dma_start(out=zb[2 * H:2 * H + 8, :], in_=b_qkv[2 * E:3 * E].rearrange("(r c) -> r c", c=P))
-            elif ld[0] == "LX":
-                j = ld[1]
-                nc.sync.dma_start(out=xp[j][:], in_=x[:, j * P:(j + 1) * P, :].rearrange("b p k -> p b k"))
-            else:
-                c = ld[1]
-                c0 = CHUNKS[c][0] * E + CHUNKS[c][1] * BK
-                for gu in range(4):
+        def load_x(j):
+            nc.sync.dma_start(out=x_raw[j][:], in_=x[:, j * P:(j + 1) * P, :].rearrange("b p k -> p b k"))
+
+        def load_w(c, passes):
+            c0 = CHUNKS[c][0] * E + CHUNKS[c][1] * BANK
+            for g in passes:
+                for u in range(2):
+                    r0 = 4 * P * g + 2 * P * u
                     nc.sync.dma_start(
-                        out=wr[c][:, 2 * gu:2 * gu + 2, :],
-                        in_=W_qkv[256 * gu:256 * gu + 256, c0:c0 + BK].rearrange("(q e) c -> q e c", e=2),
+                        out=w_raw[c][:, 4 * g + 2 * u:4 * g + 2 * u + 2, :],
+                        in_=W_qkv[r0:r0 + 2 * P, c0:c0 + BANK].rearrange("(q e) c -> q e c", e=2),
                     )
 
+        nc.sync.dma_start(out=cos16[:], in_=cos_tab.rearrange("(t p) j -> p t j", p=P))
+        nc.sync.dma_start(out=sin16[:], in_=sin_tab.rearrange("(t p) j -> p t j", p=P))
+        qk_bias = b_qkv[0:2 * E].rearrange("(r d) -> r d", d=D)
+        nc.sync.dma_start(out=bias_rows[0:2 * H, 0:R], in_=qk_bias[:, 0:R])
+        nc.sync.dma_start(out=bias_rows[0:2 * H, R:2 * R], in_=qk_bias[:, 0:R])
+        nc.sync.dma_start(out=bias_rows[0:2 * H, 2 * R:3 * R], in_=qk_bias[:, R:D])
+        nc.sync.dma_start(
+            out=bias_rows[2 * H:2 * H + 2 * FEATURE_TILES, :], in_=b_qkv[2 * E:3 * E].rearrange("(r c) -> r c", c=P)
+        )
+        load_w(0, (0,))
+        load_x(0)
+        load_w(0, (1,))
+        load_x(1)
+        load_w(4, range(PASSES))
+        load_x(2)
+        load_x(3)
+        for c in (1, 2, 5, 3):
+            load_w(c, range(PASSES))
+
         nc.vector.tensor_copy(out=ident16[:], in_=ident[:])
-        nc.vector.tensor_tensor(out=mask[:], in0=ident[:, 0:32], in1=ident[:, 64:96], op=ALU.add)
-        nc.vector.tensor_tensor(out=mask[:, 0:16], in0=mask[:, 0:16], in1=ident[:, 48:64], op=ALU.add)
-        nc.vector.tensor_tensor(out=mask[:, 16:32], in0=mask[:, 16:32], in1=ident[:, 32:48], op=ALU.add)
-        nc.vector.tensor_copy(out=cs[:, :, 0, :], in_=cos16[:])
-        nc.vector.tensor_copy(out=cs[:, :, 1, 0:16], in_=sin16[:, :, 16:32])
-        nc.vector.tensor_scalar_mul(out=cs[:, :, 1, 16:32], in0=sin16[:, :, 0:16], scalar1=-1.0)
-        nc.vector.tensor_copy(out=tab[:, :, 0:2 * R], in_=cs[:].rearrange("p t c j -> p t (c j)"))
+        nc.vector.tensor_tensor(out=mask[:], in0=ident[:, 0:R], in1=ident[:, 2 * R:3 * R], op=ALU.add)
+        nc.vector.tensor_tensor(
+            out=mask[:, 0:HALF], in0=mask[:, 0:HALF], in1=ident[:, R + HALF:2 * R], op=ALU.add
+        )
+        nc.vector.tensor_tensor(out=mask[:, HALF:R], in0=mask[:, HALF:R], in1=ident[:, R:R + HALF], op=ALU.add)
+        nc.vector.tensor_copy(out=factors[:, :, 0, :], in_=cos16[:])
+        nc.vector.tensor_copy(out=factors[:, :, 1, 0:HALF], in_=sin16[:, :, HALF:R])
+        nc.vector.tensor_scalar_mul(out=factors[:, :, 1, HALF:R], in0=sin16[:, :, 0:HALF], scalar1=-1.0)
+        nc.vector.tensor_copy(out=table[:, :, 0:2 * R], in_=factors[:].rearrange("p t c j -> p t (c j)"))
 
         live = {}
-        for st in STEPS:
-            k = st[0]
-            if k == "XT":
-                j, b = st[1], st[2]
-                xt = psum.tile([P, 4, P], F32, name="xt", tag="bank")
-                live[("xt", j, b)] = xt
-                xw = xp[j][:, b, :].bitcast(F32)
-                for gu in range(4):
-                    nc.tensor.transpose(xt[:, gu, :], xw[:, gu * P:(gu + 1) * P], ident[:])
-            elif k == "XE":
-                j, b = st[1], st[2]
-                if ("xg", j) not in live:
-                    live[("xg", j)] = xgp.tile([P, B, 2, P, 4], BF16, name="xg", tag="xg", align_bytes=64)
-                nc.scalar.copy(
-                    out=live[("xg", j)][:].bitcast(F32)[:, b],
-                    in_=live[("xt", j, b)][:].rearrange("p (g u) r -> p g r u", u=2),
+
+        def mx_product(out, lhsT, lhsT_scale, rhs, rhs_scale):
+            for g in range(PASSES):
+                nc.tensor.matmul_mx(
+                    out=out,
+                    lhsT=lhsT(g).bitcast(FP8X4),
+                    lhsT_scale=lhsT_scale(g),
+                    rhs=rhs(g).bitcast(FP8X4),
+                    rhs_scale=rhs_scale(g),
+                    start=(g == 0),
+                    stop=(g == PASSES - 1),
                 )
-            elif k == "XQ":
-                j = st[1]
-                for b in range(B):
-                    for g in range(2):
-                        nc.vector.quantize_mx(
-                            out=xc[:, b, g, j, :].bitcast(FP8X4),
-                            scales=xs[:, b, g, j, :],
-                            in_=live[("xg", j)][:, b, g].rearrange("p r t -> p (r t)"),
-                        )
-            elif k == "RG" or k == "RH":
-                c, g = st[1], st[2]
-                if ("wg", c) not in live:
-                    live[("wg", c)] = wgp.tile([P, 2, BK, 4], BF16, name="wg", tag="wg", align_bytes=64)
-                lo, hi = 0, BK
-                if k == "RH":
-                    lo, hi = st[3] * (BK // 2), (st[3] + 1) * (BK // 2)
-                dst = live[("wg", c)][:, g, lo:hi, :].rearrange("p (c i) t -> p c t i", i=4)
-                src = wr[c][:, 4 * g:4 * g + 4, lo:hi].rearrange("p t (c i) -> p c t i", i=4)
-                if k == "RG":
+
+        def x_T(j):
+            for b in range(B):
+                words = x_raw[j][:, b, :].bitcast(F32)
+                bank = psum.tile([P, 2 * PASSES, P], F32, name="x_bank", tag="bank")
+                live[("x_bank", j, b)] = bank
+                for gu in range(2 * PASSES):
+                    nc.tensor.transpose(bank[:, gu, :], words[:, gu * P:(gu + 1) * P], ident[:])
+
+        def x_out(j):
+            live[("x_grouped", j)] = x_grouped_pool.tile(
+                [P, B, PASSES, P, 4], BF16, name="x_grouped", tag="x_grouped", align_bytes=64
+            )
+            for b in range(B):
+                nc.scalar.copy(
+                    out=live[("x_grouped", j)][:].bitcast(F32)[:, b],
+                    in_=live[("x_bank", j, b)][:].rearrange("p (g u) r -> p g r u", u=2),
+                )
+
+        def x_quant(j):
+            for b in range(B):
+                for g in range(PASSES):
+                    nc.vector.quantize_mx(
+                        out=x_codes[:, b, g, j, :].bitcast(FP8X4),
+                        scales=x_scales[:, b, g, j, :],
+                        in_=live[("x_grouped", j)][:, b, g].rearrange("p r t -> p (r t)"),
+                    )
+
+        def regroup(engine, c, g):
+            if ("w_grouped", c) not in live:
+                live[("w_grouped", c)] = w_grouped_pool.tile(
+                    [P, PASSES, BANK, 4], BF16, name="w_grouped", tag="w_grouped", align_bytes=64
+                )
+            pieces = 1 if engine == VECTOR else 2
+            width = BANK // pieces
+            for i in range(pieces):
+                dst = live[("w_grouped", c)][:, g, i * width:(i + 1) * width, :]
+                src = w_raw[c][:, 4 * g:4 * g + 4, i * width:(i + 1) * width]
+                dst = dst.rearrange("p (c i) t -> p c t i", i=4)
+                src = src.rearrange("p t (c i) -> p c t i", i=4)
+                if engine == VECTOR:
                     nc.vector.tensor_copy(out=dst, in_=src)
                 else:
                     nc.scalar.copy(out=dst, in_=src)
-            elif k == "WQ":
-                c = st[1]
-                nc.vector.quantize_mx(
-                    out=wc[c][:].rearrange("p g c -> p (g c)").bitcast(FP8X4),
-                    scales=ws[c][:].rearrange("p g c -> p (g c)"),
-                    in_=live[("wg", c)][:].rearrange("p g c t -> p (g c t)"),
-                )
-            elif k == "ST1":
-                tps = psum.tile([P, NPT, P], BF16, name="tps", tag="bank")
-                for t in range(NPT):
-                    nc.tensor.transpose(tps[:, t, :], tab[:, t, :], ident16[:])
-                zps = psum.tile([P, P], BF16, name="zps", tag="bank")
-                nc.tensor.transpose(zps[:], zb[:], ident16[:])
-                live["tps"] = tps
-                live["zps"] = zps
-            elif k == "BBP":
-                w = st[1]
-                pb = psum.tile([P, H, R], F32, name="pb", tag="bank")
-                live[("pb", w)] = pb
+
+        def w_quant(c):
+            nc.vector.quantize_mx(
+                out=w_codes[c][:].rearrange("p g c -> p (g c)").bitcast(FP8X4),
+                scales=w_scales[c][:].rearrange("p g c -> p (g c)"),
+                in_=live[("w_grouped", c)][:].rearrange("p g c t -> p (g c t)"),
+            )
+
+        def tables_T():
+            bank = psum.tile([P, TILES, P], BF16, name="table_bank", tag="bank")
+            live["table_bank"] = bank
+            for t in range(TILES):
+                nc.tensor.transpose(bank[:, t, :], table[:, t, :], ident16[:])
+            bank = psum.tile([P, P], BF16, name="bias_bank", tag="bank")
+            live["bias_bank"] = bank
+            nc.tensor.transpose(bank[:], bias_rows[:], ident16[:])
+
+        def tables_out():
+            nc.scalar.copy(out=table_T[:], in_=live["table_bank"][:])
+
+        def bias_mask():
+            nc.vector.tensor_tensor(
+                out=bias_masked[:],
+                in0=live["bias_bank"][:, 0:2 * H].unsqueeze(2).to_broadcast([P, 2 * H, R]),
+                in1=mask[:].unsqueeze(1).to_broadcast([P, 2 * H, R]),
+                op=ALU.mult,
+            )
+            nc.vector.tensor_copy(out=v_bias[:], in_=live["bias_bank"][:, 2 * H:2 * H + 2 * FEATURE_TILES])
+
+        def bias_mm():
+            for w in range(2):
+                bank = psum.tile([P, H, R], F32, name="pass_bank", tag="bank")
+                live[("pass_bank", w)] = bank
                 nc.tensor.matmul(
-                    out=pb[:].rearrange("p h j -> p (h j)"),
-                    lhsT=sel[:],
-                    rhs=bmat[:, w * H:(w + 1) * H, :].rearrange("p r j -> p (r j)"),
+                    out=bank[:].rearrange("p h j -> p (h j)"),
+                    lhsT=selector[:],
+                    rhs=bias_masked[:, w * H:(w + 1) * H, :].rearrange("p r j -> p (r j)"),
                     start=True,
                     stop=True,
                 )
-            elif k == "BBS":
-                w = st[1]
-                nc.scalar.copy(out=bias[:, w * H:(w + 1) * H, :], in_=live[("pb", w)][:])
-            elif k == "TABT":
-                nc.scalar.copy(out=tabT[:], in_=live["tps"][:])
-            elif k == "BMAT":
+
+        def bias_out():
+            for w in range(2):
+                nc.scalar.copy(out=pass_bias[:, w * H:(w + 1) * H, :], in_=live[("pass_bank", w)][:])
+
+        def unit_mm(unit):
+            c, j = unit // TILES, unit % TILES
+            head0 = CHUNKS[c][0] * H + CHUNKS[c][1] * HEADS
+            bank = psum.tile([P, HEADS, R], F32, name="turned_bank", tag="bank")
+            live[("turned_bank", unit)] = bank
+            nc.tensor.matmul(
+                out=bank[:].rearrange("p h j -> p (h j)"),
+                lhsT=table_T[:, j, :],
+                rhs=bias_masked[:, head0:head0 + HEADS, :].rearrange("p r j -> p (r j)"),
+                start=True,
+                stop=True,
+            )
+            for b in range(B):
+                bank = psum.tile([P, BANK], F32, name="unit_bank", tag="bank")
+                live[("unit_bank", unit, b)] = bank
+                mx_product(
+                    bank[:],
+                    lambda g: x_codes[:, b, g, j, :],
+                    lambda g: x_scales[:, b, g, j, :],
+                    lambda g: w_codes[c][:, g, :],
+                    lambda g: w_scales[c][:, g, :],
+                )
+
+        def turned_bias_out(unit):
+            live[("turned_bias", unit)] = turned_bias_pool.tile([P, HEADS, R], F32, name="turned_bias", tag="turned_bias")
+            nc.scalar.copy(out=live[("turned_bias", unit)][:], in_=live[("turned_bank", unit)][:])
+
+        def unit_vec(unit):
+            c, j = unit // TILES, unit % TILES
+            head0 = CHUNKS[c][0] * H + CHUNKS[c][1] * HEADS
+            products = products_pool.tile([P, B, HEADS, 2, R], F32, name="products", tag="products")
+            result = unit_out_pool.tile([P, B, BANK], F32, name="unit_out", tag="unit_out")
+            live[("products", unit)] = products
+            live[("unit_out", unit)] = result
+            for b in range(B):
+                heads = live[("unit_bank", unit, b)][:].rearrange("p (h d) -> p h d", d=D)
                 nc.vector.tensor_tensor(
-                    out=bmat[:],
-                    in0=live["zps"][:, 0:2 * H].unsqueeze(2).to_broadcast([P, 2 * H, R]),
-                    in1=mask[:].unsqueeze(1).to_broadcast([P, 2 * H, R]),
+                    out=products[:, b],
+                    in0=heads[:, :, 0:R].unsqueeze(2).to_broadcast([P, HEADS, 2, R]),
+                    in1=factors[:, j].unsqueeze(1).to_broadcast([P, HEADS, 2, R]),
                     op=ALU.mult,
                 )
-                nc.vector.tensor_copy(out=bt[:], in_=live["zps"][:, 2 * H:2 * H + 8])
-            elif k in ("BP", "BS", "MX", "TA", "Y", "G", "SO"):
-                u = st[1]
-                c = TURNED[u // NPT]
-                j = u % NPT
-                which, half = CHUNKS[c]
-                c0 = which * E + half * BK
-                r0 = which * H + half * HPB
-                if k == "BP":
-                    bp = psum.tile([P, HPB, R], F32, name="bp", tag="bank")
-                    live[("bp", u)] = bp
-                    nc.tensor.matmul(
-                        out=bp[:].rearrange("p h j -> p (h j)"),
-                        lhsT=tabT[:, j, :],
-                        rhs=bmat[:, r0:r0 + HPB, :].rearrange("p r j -> p (r j)"),
-                        start=True,
-                        stop=True,
-                    )
-                elif k == "BS":
-                    live[("bs", u)] = bsp.tile([P, HPB, R], F32, name="bs", tag="bs")
-                    nc.scalar.copy(out=live[("bs", u)][:], in_=live[("bp", u)][:])
-                elif k == "MX":
-                    b = st[2]
-                    acc = psum.tile([P, BK], F32, name="acc", tag="bank")
-                    live[("acc", u, b)] = acc
-                    for g in range(2):
-                        nc.tensor.matmul_mx(
-                            out=acc[:],
-                            lhsT=xc[:, b, g, j, :].bitcast(FP8X4),
-                            lhsT_scale=xs[:, b, g, j, :],
-                            rhs=wc[c][:, g, :].bitcast(FP8X4),
-                            rhs_scale=ws[c][:, g, :],
-                            start=(g == 0),
-                            stop=(g == 1),
-                        )
-                elif k == "TA":
-                    b = st[2]
-                    if ("t", u) not in live:
-                        live[("t", u)] = tp.tile([P, B, HPB, 2, R], F32, name="t", tag="t")
-                        live[("o", u)] = op.tile([P, B, BK], F32, name="o", tag="o")
-                    av = live[("acc", u, b)][:].rearrange("p (h d) -> p h d", d=D)
-                    nc.vector.tensor_tensor(
-                        out=live[("t", u)][:, b],
-                        in0=av[:, :, 0:R].unsqueeze(2).to_broadcast([P, HPB, 2, R]),
-                        in1=cs[:, j].unsqueeze(1).to_broadcast([P, HPB, 2, R]),
-                        op=ALU.mult,
-                    )
-                    nc.vector.tensor_tensor(
-                        out=live[("o", u)][:, b, :].rearrange("p (h d) -> p h d", d=D)[:, :, R:D],
-                        in0=av[:, :, R:D],
-                        in1=bias[:, r0:r0 + HPB, :],
-                        op=ALU.add,
-                    )
-                elif k == "Y":
-                    tc0 = live[("t", u)][:, :, :, 0, :]
-                    nc.vector.tensor_tensor(
-                        out=tc0,
-                        in0=tc0,
-                        in1=live[("bp", u)][:].unsqueeze(1).to_broadcast([P, B, HPB, R]),
-                        op=ALU.add,
-                    )
-                elif k == "G":
-                    o = live[("o", u)]
-                    ov = o[:].rearrange("p b (h d) -> p (b h) d", d=D)
-                    tv = live[("t", u)][:].rearrange("p b h c j -> p (b h) c j")
-                    nc.gpsimd.tensor_tensor(
-                        out=ov[:, :, 0:16], in0=tv[:, :, 0, 0:16], in1=tv[:, :, 1, 16:32], op=ALU.add
-                    )
-                    nc.gpsimd.tensor_tensor(
-                        out=ov[:, :, 16:32], in0=tv[:, :, 0, 16:32], in1=tv[:, :, 1, 0:16], op=ALU.add
-                    )
-                    if u not in FROM_PSUM:
-                        o4 = o[:].rearrange("p b (h d) -> p b h d", d=D)[:, :, :, 0:R]
-                        nc.gpsimd.tensor_tensor(
-                            out=o4,
-                            in0=o4,
-                            in1=live[("bs", u)][:].unsqueeze(1).to_broadcast([P, B, HPB, R]),
-                            op=ALU.add,
-                        )
-                else:
-                    dst = outs[which].rearrange("b s h d -> s b (h d)")
-                    nc.sync.dma_start(
-                        out=dst[j * P:(j + 1) * P, :, half * BK:(half + 1) * BK], in_=live[("o", u)][:]
-                    )
+                nc.vector.tensor_tensor(
+                    out=result[:, b, :].rearrange("p (h d) -> p h d", d=D)[:, :, R:D],
+                    in0=heads[:, :, R:D],
+                    in1=pass_bias[:, head0:head0 + HEADS, :],
+                    op=ALU.add,
+                )
+            if vector_adds_turned_bias(unit):
+                with_cos = products[:, :, :, 0, :]
+                nc.vector.tensor_tensor(
+                    out=with_cos,
+                    in0=with_cos,
+                    in1=live[("turned_bank", unit)][:].unsqueeze(1).to_broadcast([P, B, HEADS, R]),
+                    op=ALU.add,
+                )
+
+        def unit_add(unit):
+            result = live[("unit_out", unit)]
+            heads = result[:].rearrange("p b (h d) -> p (b h) d", d=D)
+            products = live[("products", unit)][:].rearrange("p b h c j -> p (b h) c j")
+            nc.gpsimd.tensor_tensor(
+                out=heads[:, :, 0:HALF], in0=products[:, :, 0, 0:HALF], in1=products[:, :, 1, HALF:R], op=ALU.add
+            )
+            nc.gpsimd.tensor_tensor(
+                out=heads[:, :, HALF:R], in0=products[:, :, 0, HALF:R], in1=products[:, :, 1, 0:HALF], op=ALU.add
+            )
+            if not vector_adds_turned_bias(unit):
+                turned = result[:].rearrange("p b (h d) -> p b h d", d=D)[:, :, :, 0:R]
+                nc.gpsimd.tensor_tensor(
+                    out=turned,
+                    in0=turned,
+                    in1=live[("turned_bias", unit)][:].unsqueeze(1).to_broadcast([P, B, HEADS, R]),
+                    op=ALU.add,
+                )
+
+        def unit_store(unit):
+            c, j = unit // TILES, unit % TILES
+            which, half = CHUNKS[c]
+            dst = outs[which].rearrange("b s h d -> s b (h d)")
+            nc.sync.dma_start(
+                out=dst[j * P:(j + 1) * P, :, half * BANK:(half + 1) * BANK], in_=live[("unit_out", unit)][:]
+            )
+
+        def v_mm(pair):
+            for n in (2 * pair, 2 * pair + 1):
+                c, b, f = V_CHUNKS[n // 8], (n // FEATURE_TILES) % B, n % FEATURE_TILES
+                bank = psum.tile([P, BANK], F32, name="v_bank", tag="bank")
+                live[("v_bank", n)] = bank
+                mx_product(
+                    bank[:],
+                    lambda g: w_codes[c][:, g, f * P:(f + 1) * P],
+                    lambda g: w_scales[c][:, g, f * P:(f + 1) * P],
+                    lambda g: x_codes[:, b, g].rearrange("p j r -> p (j r)"),
+                    lambda g: x_scales[:, b, g].rearrange("p j r -> p (j r)"),
+                )
+
+        def v_bias_add(pair):
+            for n in (2 * pair, 2 * pair + 1):
+                column = CHUNKS[V_CHUNKS[n // 8]][1] * FEATURE_TILES + n % FEATURE_TILES
+                live[("v_T", n)] = v_T_pool.tile([P, BANK], F32, name="v_T", tag="v_T")
+                nc.scalar.activation(
+                    out=live[("v_T", n)][:],
+                    in_=live[("v_bank", n)][:],
+                    func=ACT.Identity,
+                    bias=v_bias[:, column:column + 1],
+                    scale=1.0,
+                )
+
+        def v_T(pair):
+            for n in (2 * pair, 2 * pair + 1):
+                bank = psum.tile([P, TILES, P], F32, name="v_back", tag="bank")
+                live[("v_back", n)] = bank
+                for j in range(TILES):
+                    nc.tensor.transpose(bank[:, j, :], live[("v_T", n)][:, j * P:(j + 1) * P], ident[:])
+
+        def v_out(pair):
+            for n in (2 * pair, 2 * pair + 1):
+                group, f = n // FEATURE_TILES, n % FEATURE_TILES
+                if f == 0:
+                    live[("v_out", group)] = v_out_pool.tile([P, TILES, BANK], F32, name="v_out", tag="v_out")
+                nc.scalar.copy(out=live[("v_out", group)][:, :, f * P:(f + 1) * P], in_=live[("v_back", n)][:])
+
+        def v_store(group):
+            half, b = CHUNKS[V_CHUNKS[group // B]][1], group % B
+            dst = out_2.rearrange("b (j p) h d -> p b j (h d)", p=P)
+            nc.sync.dma_start(out=dst[:, b, :, half * BANK:(half + 1) * BANK], in_=live[("v_out", group)][:])
+
+        writers = {
+            "x_T": x_T, "x_out": x_out, "x_quant": x_quant, "w_quant": w_quant, "unit_mm": unit_mm,
+            "turned_bias_out": turned_bias_out, "unit_vec": unit_vec, "unit_add": unit_add, "unit_store": unit_store,
+            "v_mm": v_mm, "v_bias": v_bias_add, "v_T": v_T, "v_out": v_out, "v_store": v_store,
+        }
+        once = {"tables_T": tables_T, "tables_out": tables_out, "bias_mask": bias_mask, "bias_mm": bias_mm,
+                "bias_out": bias_out}
+        for engine, step in text_order():
+            if step[0] == "regroup":
+                regroup(engine, step[1], step[2])
+            elif step[0] in once:
+                once[step[0]]()
             else:
-                n = st[1]
-                if k == "SV":
-                    c = PLAIN[n // 2]
-                    b = n % 2
-                    half = CHUNKS[c][1]
-                    dst = out_2.rearrange("b (j p) h d -> p b j (h d)", p=P)
-                    nc.sync.dma_start(out=dst[:, b, :, half * BK:(half + 1) * BK], in_=live[("ovt", n)][:])
-                else:
-                    c = PLAIN[n // 8]
-                    b = (n // 4) % 2
-                    ft = n % 4
-                    half = CHUNKS[c][1]
-                    if k == "VP":
-                        acct = psum.tile([P, BK], F32, name="acct", tag="bank")
-                        live[("at", n)] = acct
-                        for g in range(2):
-                            nc.tensor.matmul_mx(
-                                out=acct[:],
-                                lhsT=wc[c][:, g, ft * P:(ft + 1) * P].bitcast(FP8X4),
-                                lhsT_scale=ws[c][:, g, ft * P:(ft + 1) * P],
-                                rhs=xc[:, b, g].rearrange("p j r -> p (j r)").bitcast(FP8X4),
-                                rhs_scale=xs[:, b, g].rearrange("p j r -> p (j r)"),
-                                start=(g == 0),
-                                stop=(g == 1),
-                            )
-                    elif k == "VS":
-                        live[("vt", n)] = vtp.tile([P, BK], F32, name="vt", tag="vt")
-                        nc.scalar.activation(
-                            out=live[("vt", n)][:],
-                            in_=live[("at", n)][:],
-                            func=ACT.Identity,
-                            bias=bt[:, half * 4 + ft:half * 4 + ft + 1],
-                            scale=1.0,
-                        )
-                    elif k == "WP":
-                        tb = psum.tile([P, NPT, P], F32, name="tb", tag="bank")
-                        live[("tb", n)] = tb
-                        for j in range(NPT):
-                            nc.tensor.transpose(tb[:, j, :], live[("vt", n)][:, j * P:(j + 1) * P], ident[:])
-                    else:
-                        if ("ovt", n // 4) not in live:
-                            live[("ovt", n // 4)] = vop.tile([P, NPT, BK], F32, name="ovt", tag="ovt")
-                        nc.scalar.copy(
-                            out=live[("ovt", n // 4)][:, :, ft * P:(ft + 1) * P], in_=live[("tb", n)][:]
-                        )
+                writers[step[0]](step[1])

@@ -28,116 +28,11 @@ UNITS = 4 * TILES
 V_STEPS = 16
 V_PAIRS = V_STEPS // 2
 FEATURE_TILES = BANK // P
-VECTOR = 2
+STEPS_PER_CHUNK = B * FEATURE_TILES
 
 
 def vector_adds_turned_bias(unit):
     return unit % 2 == 0 or unit == UNITS - 1
-
-
-def engine_orders():
-    v_halves = []
-    for pair in range(V_PAIRS + 1):
-        if pair < V_PAIRS:
-            v_halves.append(("front", pair))
-        if pair >= 1:
-            v_halves.append(("back", pair - 1))
-
-    tensor = [("tables_T",), ("x_T", 0), ("bias_mm",), ("x_T", 1), ("unit_mm", 0), ("unit_mm", 1),
-              ("x_T", 2), ("x_T", 3), ("unit_mm", 2), ("unit_mm", 3)]
-    scalar = [("tables_out",), ("x_out", 0), ("bias_out",), ("x_out", 1), ("regroup", 4, 0), ("x_out", 2),
-              ("x_out", 3), ("regroup", 4, 1)]
-    for unit in range(4):
-        if not vector_adds_turned_bias(unit):
-            scalar.append(("turned_bias_out", unit))
-    late_regroups = [(c, g) for c in (1, 2, 5, 3) for g in range(PASSES)]
-    for c, g in late_regroups[:4]:
-        scalar.append(("regroup", c, g))
-    late_regroups = late_regroups[4:]
-    written = 0
-    for unit in range(4, UNITS + 1):
-        if unit < UNITS:
-            tensor.append(("unit_mm", unit))
-            if not vector_adds_turned_bias(unit):
-                scalar.append(("turned_bias_out", unit))
-        due = min(len(v_halves), (3 * (unit - 4) + 1) // 2)
-        while written < due:
-            half, pair = v_halves[written]
-            tensor.append(("v_mm" if half == "front" else "v_T", pair))
-            scalar.append(("v_bias" if half == "front" else "v_out", pair))
-            if late_regroups and written % 2 == 0:
-                scalar.append(("regroup",) + late_regroups[0])
-                late_regroups = late_regroups[1:]
-            written += 1
-
-    vector = [("bias_mask",), ("regroup", 0, 0), ("regroup", 0, 1), ("x_quant", 0), ("w_quant", 0), ("x_quant", 1),
-              ("unit_vec", 0), ("unit_vec", 1), ("x_quant", 2), ("x_quant", 3)]
-    quantise_after = {3: (4, 1), 6: (2,), 8: (5,), 10: (3,)}
-    for unit in range(2, UNITS):
-        vector.append(("unit_vec", unit))
-        for c in quantise_after.get(unit, ()):
-            vector.append(("w_quant", c))
-
-    gpsimd = [("unit_add", unit) for unit in range(UNITS)]
-
-    v_store_after = {7: 0, 10: 1, 12: 2, 14: 3}
-    sync = []
-    for unit in range(UNITS):
-        sync.append(("unit_store", unit))
-        if unit in v_store_after:
-            sync.append(("v_store", v_store_after[unit]))
-    return [tensor, scalar, vector, gpsimd, sync]
-
-
-def needs(step):
-    kind = step[0]
-    n = step[1] if len(step) > 1 else 0
-    if kind == "x_out":
-        return [("x_T", n)]
-    if kind == "x_quant":
-        return [("x_out", n)]
-    if kind in ("tables_out", "bias_mask"):
-        return [("tables_T",)]
-    if kind == "bias_mm":
-        return [("bias_mask",)]
-    if kind == "bias_out":
-        return [("bias_mm",)]
-    if kind == "w_quant":
-        return [("regroup", n, g) for g in range(PASSES)]
-    if kind == "unit_mm":
-        return [("tables_out",), ("bias_mask",), ("x_quant", n % TILES), ("w_quant", n // TILES)]
-    if kind == "turned_bias_out":
-        return [("unit_mm", n)]
-    if kind == "unit_vec":
-        return [("unit_mm", n), ("bias_out",)]
-    if kind == "unit_add":
-        return [("unit_vec", n)] + ([] if vector_adds_turned_bias(n) else [("turned_bias_out", n)])
-    if kind == "unit_store":
-        return [("unit_add", n)]
-    if kind == "v_mm":
-        return [("w_quant", V_CHUNKS[n // (V_PAIRS // 2)])] + [("x_quant", j) for j in range(TILES)]
-    if kind == "v_bias":
-        return [("v_mm", n), ("bias_mask",)]
-    if kind == "v_T":
-        return [("v_bias", n)]
-    if kind == "v_out":
-        return [("v_T", n)]
-    if kind == "v_store":
-        return [("v_out", 2 * n + 1)]
-    return []
-
-
-def text_order():
-    queues = engine_orders()
-    written = set()
-    order = []
-    while any(queues):
-        for q in range(len(queues)):
-            if queues[q] and all(s in written for s in needs(queues[q][0])):
-                order.append((q, queues[q][0]))
-                written.add(queues[q][0])
-                queues[q] = queues[q][1:]
-    return order
 
 
 def tile_improvedattention_pa_kernel(tc, x, W_qkv, b_qkv, sin_tab, cos_tab, out_0, out_1, out_2):
@@ -224,8 +119,6 @@ def tile_improvedattention_pa_kernel(tc, x, W_qkv, b_qkv, sin_tab, cos_tab, out_
         nc.vector.tensor_scalar_mul(out=factors[:, :, 1, HALF:R], in0=sin16[:, :, 0:HALF], scalar1=-1.0)
         nc.vector.tensor_copy(out=table[:, :, 0:2 * R], in_=factors[:].rearrange("p t c j -> p t (c j)"))
 
-        live = {}
-
         def mx_product(out, lhsT, lhsT_scale, rhs, rhs_scale):
             for g in range(PASSES):
                 nc.tensor.matmul_mx(
@@ -238,109 +131,65 @@ def tile_improvedattention_pa_kernel(tc, x, W_qkv, b_qkv, sin_tab, cos_tab, out_
                     stop=(g == PASSES - 1),
                 )
 
-        def x_T(j):
+        def transpose_x(j):
+            grouped = x_grouped_pool.tile([P, B, PASSES, P, 4], BF16, name="x_grouped", tag="x_grouped", align_bytes=64)
+            banks = []
             for b in range(B):
                 words = x_raw[j][:, b, :].bitcast(F32)
                 bank = psum.tile([P, 2 * PASSES, P], F32, name="x_bank", tag="bank")
-                live[("x_bank", j, b)] = bank
                 for gu in range(2 * PASSES):
                     nc.tensor.transpose(bank[:, gu, :], words[:, gu * P:(gu + 1) * P], ident[:])
-
-        def x_out(j):
-            live[("x_grouped", j)] = x_grouped_pool.tile(
-                [P, B, PASSES, P, 4], BF16, name="x_grouped", tag="x_grouped", align_bytes=64
-            )
+                banks.append(bank)
             for b in range(B):
                 nc.scalar.copy(
-                    out=live[("x_grouped", j)][:].bitcast(F32)[:, b],
-                    in_=live[("x_bank", j, b)][:].rearrange("p (g u) r -> p g r u", u=2),
+                    out=grouped[:].bitcast(F32)[:, b], in_=banks[b][:].rearrange("p (g u) r -> p g r u", u=2)
                 )
+            return grouped
 
-        def x_quant(j):
+        def quantise_x(j, grouped):
             for b in range(B):
                 for g in range(PASSES):
                     nc.vector.quantize_mx(
                         out=x_codes[:, b, g, j, :].bitcast(FP8X4),
                         scales=x_scales[:, b, g, j, :],
-                        in_=live[("x_grouped", j)][:, b, g].rearrange("p r t -> p (r t)"),
+                        in_=grouped[:, b, g].rearrange("p r t -> p (r t)"),
                     )
 
-        def regroup(engine, c, g):
-            if ("w_grouped", c) not in live:
-                live[("w_grouped", c)] = w_grouped_pool.tile(
+        w_grouped = {}
+
+        def regroup_w(copy, pieces, c, g):
+            if g == 0:
+                w_grouped[c] = w_grouped_pool.tile(
                     [P, PASSES, BANK, 4], BF16, name="w_grouped", tag="w_grouped", align_bytes=64
                 )
-            pieces = 1 if engine == VECTOR else 2
             width = BANK // pieces
             for i in range(pieces):
-                dst = live[("w_grouped", c)][:, g, i * width:(i + 1) * width, :]
-                src = w_raw[c][:, 4 * g:4 * g + 4, i * width:(i + 1) * width]
-                dst = dst.rearrange("p (c i) t -> p c t i", i=4)
-                src = src.rearrange("p t (c i) -> p c t i", i=4)
-                if engine == VECTOR:
-                    nc.vector.tensor_copy(out=dst, in_=src)
-                else:
-                    nc.scalar.copy(out=dst, in_=src)
+                copy(
+                    out=w_grouped[c][:, g, i * width:(i + 1) * width, :].rearrange("p (c i) t -> p c t i", i=4),
+                    in_=w_raw[c][:, 4 * g:4 * g + 4, i * width:(i + 1) * width].rearrange("p t (c i) -> p c t i", i=4),
+                )
 
-        def w_quant(c):
+        def quantise_w(c):
             nc.vector.quantize_mx(
                 out=w_codes[c][:].rearrange("p g c -> p (g c)").bitcast(FP8X4),
                 scales=w_scales[c][:].rearrange("p g c -> p (g c)"),
-                in_=live[("w_grouped", c)][:].rearrange("p g c t -> p (g c t)"),
+                in_=w_grouped[c][:].rearrange("p g c t -> p (g c t)"),
             )
 
-        def tables_T():
-            bank = psum.tile([P, TILES, P], BF16, name="table_bank", tag="bank")
-            live["table_bank"] = bank
-            for t in range(TILES):
-                nc.tensor.transpose(bank[:, t, :], table[:, t, :], ident16[:])
-            bank = psum.tile([P, P], BF16, name="bias_bank", tag="bank")
-            live["bias_bank"] = bank
-            nc.tensor.transpose(bank[:], bias_rows[:], ident16[:])
-
-        def tables_out():
-            nc.scalar.copy(out=table_T[:], in_=live["table_bank"][:])
-
-        def bias_mask():
-            nc.vector.tensor_tensor(
-                out=bias_masked[:],
-                in0=live["bias_bank"][:, 0:2 * H].unsqueeze(2).to_broadcast([P, 2 * H, R]),
-                in1=mask[:].unsqueeze(1).to_broadcast([P, 2 * H, R]),
-                op=ALU.mult,
-            )
-            nc.vector.tensor_copy(out=v_bias[:], in_=live["bias_bank"][:, 2 * H:2 * H + 2 * FEATURE_TILES])
-
-        def bias_mm():
-            for w in range(2):
-                bank = psum.tile([P, H, R], F32, name="pass_bank", tag="bank")
-                live[("pass_bank", w)] = bank
-                nc.tensor.matmul(
-                    out=bank[:].rearrange("p h j -> p (h j)"),
-                    lhsT=selector[:],
-                    rhs=bias_masked[:, w * H:(w + 1) * H, :].rearrange("p r j -> p (r j)"),
-                    start=True,
-                    stop=True,
-                )
-
-        def bias_out():
-            for w in range(2):
-                nc.scalar.copy(out=pass_bias[:, w * H:(w + 1) * H, :], in_=live[("pass_bank", w)][:])
-
-        def unit_mm(unit):
+        def unit_products(unit):
             c, j = unit // TILES, unit % TILES
             head0 = CHUNKS[c][0] * H + CHUNKS[c][1] * HEADS
-            bank = psum.tile([P, HEADS, R], F32, name="turned_bank", tag="bank")
-            live[("turned_bank", unit)] = bank
+            turned_bank = psum.tile([P, HEADS, R], F32, name="turned_bank", tag="bank")
             nc.tensor.matmul(
-                out=bank[:].rearrange("p h j -> p (h j)"),
+                out=turned_bank[:].rearrange("p h j -> p (h j)"),
                 lhsT=table_T[:, j, :],
                 rhs=bias_masked[:, head0:head0 + HEADS, :].rearrange("p r j -> p (r j)"),
                 start=True,
                 stop=True,
             )
+            banks = []
             for b in range(B):
                 bank = psum.tile([P, BANK], F32, name="unit_bank", tag="bank")
-                live[("unit_bank", unit, b)] = bank
                 mx_product(
                     bank[:],
                     lambda g: x_codes[:, b, g, j, :],
@@ -348,20 +197,21 @@ def tile_improvedattention_pa_kernel(tc, x, W_qkv, b_qkv, sin_tab, cos_tab, out_
                     lambda g: w_codes[c][:, g, :],
                     lambda g: w_scales[c][:, g, :],
                 )
+                banks.append(bank)
+            turned_bias = turned_bank
+            if not vector_adds_turned_bias(unit):
+                turned_bias = turned_bias_pool.tile([P, HEADS, R], F32, name="turned_bias", tag="turned_bias")
+                nc.scalar.copy(out=turned_bias[:], in_=turned_bank[:])
+            return banks, turned_bias
 
-        def turned_bias_out(unit):
-            live[("turned_bias", unit)] = turned_bias_pool.tile([P, HEADS, R], F32, name="turned_bias", tag="turned_bias")
-            nc.scalar.copy(out=live[("turned_bias", unit)][:], in_=live[("turned_bank", unit)][:])
-
-        def unit_vec(unit):
+        def unit_finish(unit, banks, turned_bias):
             c, j = unit // TILES, unit % TILES
-            head0 = CHUNKS[c][0] * H + CHUNKS[c][1] * HEADS
+            which, half = CHUNKS[c]
+            head0 = which * H + half * HEADS
             products = products_pool.tile([P, B, HEADS, 2, R], F32, name="products", tag="products")
             result = unit_out_pool.tile([P, B, BANK], F32, name="unit_out", tag="unit_out")
-            live[("products", unit)] = products
-            live[("unit_out", unit)] = result
             for b in range(B):
-                heads = live[("unit_bank", unit, b)][:].rearrange("p (h d) -> p h d", d=D)
+                heads = banks[b][:].rearrange("p (h d) -> p h d", d=D)
                 nc.vector.tensor_tensor(
                     out=products[:, b],
                     in0=heads[:, :, 0:R].unsqueeze(2).to_broadcast([P, HEADS, 2, R]),
@@ -374,47 +224,32 @@ def tile_improvedattention_pa_kernel(tc, x, W_qkv, b_qkv, sin_tab, cos_tab, out_
                     in1=pass_bias[:, head0:head0 + HEADS, :],
                     op=ALU.add,
                 )
+            for_both = turned_bias[:].unsqueeze(1).to_broadcast([P, B, HEADS, R])
             if vector_adds_turned_bias(unit):
                 with_cos = products[:, :, :, 0, :]
-                nc.vector.tensor_tensor(
-                    out=with_cos,
-                    in0=with_cos,
-                    in1=live[("turned_bank", unit)][:].unsqueeze(1).to_broadcast([P, B, HEADS, R]),
-                    op=ALU.add,
-                )
-
-        def unit_add(unit):
-            result = live[("unit_out", unit)]
+                nc.vector.tensor_tensor(out=with_cos, in0=with_cos, in1=for_both, op=ALU.add)
             heads = result[:].rearrange("p b (h d) -> p (b h) d", d=D)
-            products = live[("products", unit)][:].rearrange("p b h c j -> p (b h) c j")
+            pairs = products[:].rearrange("p b h c j -> p (b h) c j")
             nc.gpsimd.tensor_tensor(
-                out=heads[:, :, 0:HALF], in0=products[:, :, 0, 0:HALF], in1=products[:, :, 1, HALF:R], op=ALU.add
+                out=heads[:, :, 0:HALF], in0=pairs[:, :, 0, 0:HALF], in1=pairs[:, :, 1, HALF:R], op=ALU.add
             )
             nc.gpsimd.tensor_tensor(
-                out=heads[:, :, HALF:R], in0=products[:, :, 0, HALF:R], in1=products[:, :, 1, 0:HALF], op=ALU.add
+                out=heads[:, :, HALF:R], in0=pairs[:, :, 0, HALF:R], in1=pairs[:, :, 1, 0:HALF], op=ALU.add
             )
             if not vector_adds_turned_bias(unit):
                 turned = result[:].rearrange("p b (h d) -> p b h d", d=D)[:, :, :, 0:R]
-                nc.gpsimd.tensor_tensor(
-                    out=turned,
-                    in0=turned,
-                    in1=live[("turned_bias", unit)][:].unsqueeze(1).to_broadcast([P, B, HEADS, R]),
-                    op=ALU.add,
-                )
-
-        def unit_store(unit):
-            c, j = unit // TILES, unit % TILES
-            which, half = CHUNKS[c]
+                nc.gpsimd.tensor_tensor(out=turned, in0=turned, in1=for_both, op=ALU.add)
             dst = outs[which].rearrange("b s h d -> s b (h d)")
-            nc.sync.dma_start(
-                out=dst[j * P:(j + 1) * P, :, half * BANK:(half + 1) * BANK], in_=live[("unit_out", unit)][:]
-            )
+            nc.sync.dma_start(out=dst[j * P:(j + 1) * P, :, half * BANK:(half + 1) * BANK], in_=result[:])
 
-        def v_mm(pair):
+        v_T = {}
+        v_out = {}
+
+        def v_front(pair):
+            banks = []
             for n in (2 * pair, 2 * pair + 1):
-                c, b, f = V_CHUNKS[n // 8], (n // FEATURE_TILES) % B, n % FEATURE_TILES
+                c, b, f = V_CHUNKS[n // STEPS_PER_CHUNK], (n // FEATURE_TILES) % B, n % FEATURE_TILES
                 bank = psum.tile([P, BANK], F32, name="v_bank", tag="bank")
-                live[("v_bank", n)] = bank
                 mx_product(
                     bank[:],
                     lambda g: w_codes[c][:, g, f * P:(f + 1) * P],
@@ -422,49 +257,95 @@ def tile_improvedattention_pa_kernel(tc, x, W_qkv, b_qkv, sin_tab, cos_tab, out_
                     lambda g: x_codes[:, b, g].rearrange("p j r -> p (j r)"),
                     lambda g: x_scales[:, b, g].rearrange("p j r -> p (j r)"),
                 )
-
-        def v_bias_add(pair):
+                banks.append(bank)
             for n in (2 * pair, 2 * pair + 1):
-                column = CHUNKS[V_CHUNKS[n // 8]][1] * FEATURE_TILES + n % FEATURE_TILES
-                live[("v_T", n)] = v_T_pool.tile([P, BANK], F32, name="v_T", tag="v_T")
+                column = CHUNKS[V_CHUNKS[n // STEPS_PER_CHUNK]][1] * FEATURE_TILES + n % FEATURE_TILES
+                v_T[n] = v_T_pool.tile([P, BANK], F32, name="v_T", tag="v_T")
                 nc.scalar.activation(
-                    out=live[("v_T", n)][:],
-                    in_=live[("v_bank", n)][:],
-                    func=ACT.Identity,
-                    bias=v_bias[:, column:column + 1],
-                    scale=1.0,
+                    out=v_T[n][:], in_=banks[n % 2][:], func=ACT.Identity, bias=v_bias[:, column:column + 1], scale=1.0
                 )
 
-        def v_T(pair):
+        def v_back(pair):
+            banks = []
             for n in (2 * pair, 2 * pair + 1):
                 bank = psum.tile([P, TILES, P], F32, name="v_back", tag="bank")
-                live[("v_back", n)] = bank
                 for j in range(TILES):
-                    nc.tensor.transpose(bank[:, j, :], live[("v_T", n)][:, j * P:(j + 1) * P], ident[:])
-
-        def v_out(pair):
+                    nc.tensor.transpose(bank[:, j, :], v_T[n][:, j * P:(j + 1) * P], ident[:])
+                banks.append(bank)
             for n in (2 * pair, 2 * pair + 1):
-                group, f = n // FEATURE_TILES, n % FEATURE_TILES
+                quarter, f = n // FEATURE_TILES, n % FEATURE_TILES
                 if f == 0:
-                    live[("v_out", group)] = v_out_pool.tile([P, TILES, BANK], F32, name="v_out", tag="v_out")
-                nc.scalar.copy(out=live[("v_out", group)][:, :, f * P:(f + 1) * P], in_=live[("v_back", n)][:])
+                    v_out[quarter] = v_out_pool.tile([P, TILES, BANK], F32, name="v_out", tag="v_out")
+                nc.scalar.copy(out=v_out[quarter][:, :, f * P:(f + 1) * P], in_=banks[n % 2][:])
+                if f == FEATURE_TILES - 1:
+                    half, b = CHUNKS[V_CHUNKS[quarter // B]][1], quarter % B
+                    dst = out_2.rearrange("b (j p) h d -> p b j (h d)", p=P)
+                    nc.sync.dma_start(out=dst[:, b, :, half * BANK:(half + 1) * BANK], in_=v_out[quarter][:])
 
-        def v_store(group):
-            half, b = CHUNKS[V_CHUNKS[group // B]][1], group % B
-            dst = out_2.rearrange("b (j p) h d -> p b j (h d)", p=P)
-            nc.sync.dma_start(out=dst[:, b, :, half * BANK:(half + 1) * BANK], in_=live[("v_out", group)][:])
+        table_bank = psum.tile([P, TILES, P], BF16, name="table_bank", tag="bank")
+        for t in range(TILES):
+            nc.tensor.transpose(table_bank[:, t, :], table[:, t, :], ident16[:])
+        bias_bank = psum.tile([P, P], BF16, name="bias_bank", tag="bank")
+        nc.tensor.transpose(bias_bank[:], bias_rows[:], ident16[:])
+        nc.scalar.copy(out=table_T[:], in_=table_bank[:])
+        nc.vector.tensor_tensor(
+            out=bias_masked[:],
+            in0=bias_bank[:, 0:2 * H].unsqueeze(2).to_broadcast([P, 2 * H, R]),
+            in1=mask[:].unsqueeze(1).to_broadcast([P, 2 * H, R]),
+            op=ALU.mult,
+        )
+        nc.vector.tensor_copy(out=v_bias[:], in_=bias_bank[:, 2 * H:2 * H + 2 * FEATURE_TILES])
+        x_grouped = {0: transpose_x(0)}
+        pass_banks = []
+        for w in range(2):
+            pass_bank = psum.tile([P, H, R], F32, name="pass_bank", tag="bank")
+            nc.tensor.matmul(
+                out=pass_bank[:].rearrange("p h j -> p (h j)"),
+                lhsT=selector[:],
+                rhs=bias_masked[:, w * H:(w + 1) * H, :].rearrange("p r j -> p (r j)"),
+                start=True,
+                stop=True,
+            )
+            pass_banks.append(pass_bank)
+        for w in range(2):
+            nc.scalar.copy(out=pass_bias[:, w * H:(w + 1) * H, :], in_=pass_banks[w][:])
+        for g in range(PASSES):
+            regroup_w(nc.vector.tensor_copy, 1, 0, g)
+        quantise_x(0, x_grouped[0])
+        quantise_w(0)
+        x_grouped[1] = transpose_x(1)
+        quantise_x(1, x_grouped[1])
 
-        writers = {
-            "x_T": x_T, "x_out": x_out, "x_quant": x_quant, "w_quant": w_quant, "unit_mm": unit_mm,
-            "turned_bias_out": turned_bias_out, "unit_vec": unit_vec, "unit_add": unit_add, "unit_store": unit_store,
-            "v_mm": v_mm, "v_bias": v_bias_add, "v_T": v_T, "v_out": v_out, "v_store": v_store,
-        }
-        once = {"tables_T": tables_T, "tables_out": tables_out, "bias_mask": bias_mask, "bias_mm": bias_mm,
-                "bias_out": bias_out}
-        for engine, step in text_order():
-            if step[0] == "regroup":
-                regroup(engine, step[1], step[2])
-            elif step[0] in once:
-                once[step[0]]()
-            else:
-                writers[step[0]](step[1])
+        scalar_passes = [(c, g) for c in (4, 1, 2, 5, 3) for g in range(PASSES)]
+        v_parts = []
+        for pair in range(V_PAIRS + 1):
+            if pair < V_PAIRS:
+                v_parts.append(("front", pair))
+            if pair >= 1:
+                v_parts.append(("back", pair - 1))
+        quantise_after = {3: (4, 1), 6: (2,), 8: (5,), 10: (3,)}
+        placed = 0
+        for unit in range(UNITS):
+            banks, turned_bias = unit_products(unit)
+            if unit == 1:
+                for j in (2, 3):
+                    x_grouped[j] = transpose_x(j)
+            for i in range((1, 1, 2, 2)[unit] if unit < 4 else 0):
+                regroup_w(nc.scalar.copy, 2, scalar_passes[0][0], scalar_passes[0][1])
+                scalar_passes = scalar_passes[1:]
+            while placed < min(len(v_parts), (3 * (unit - 4) + 1) // 2):
+                part, pair = v_parts[placed]
+                if part == "front":
+                    v_front(pair)
+                else:
+                    v_back(pair)
+                if scalar_passes and placed % 2 == 0:
+                    regroup_w(nc.scalar.copy, 2, scalar_passes[0][0], scalar_passes[0][1])
+                    scalar_passes = scalar_passes[1:]
+                placed += 1
+            unit_finish(unit, banks, turned_bias)
+            if unit == 1:
+                for j in (2, 3):
+                    quantise_x(j, x_grouped[j])
+            for c in quantise_after.get(unit, ()):
+                quantise_w(c)

from contextlib import ExitStack

import concourse.mybir as mybir
from concourse.masks import make_identity

F32 = mybir.dt.float32
BF16 = mybir.dt.bfloat16
U32 = mybir.dt.uint32
U8 = mybir.dt.uint8
FP8X4 = mybir.dt.float8_e4m3fn_x4
ALU = mybir.AluOpType
ACT = mybir.ActivationFunctionType

P = 128
B, S, H, D = 2, 512, 16, 64
E = H * D
R = D // 2
HALF = R // 2
TILES = S // P
PASSES = E // (4 * P)
BANK = 512
HEADS = BANK // D
FLOPS = 2 * B * S * E * 3 * E

CHUNKS = ((0, 0), (0, 1), (1, 0), (1, 1), (2, 0), (2, 1))
V_CHUNKS = (4, 5)
UNITS = 4 * TILES
V_STEPS = 16
V_PAIRS = V_STEPS // 2
FEATURE_TILES = BANK // P
STEPS_PER_CHUNK = B * FEATURE_TILES


def vector_adds_turned_bias(unit):
    return unit % 2 == 0 or unit == UNITS - 1


def tile_improvedattention_pa_kernel(tc, x, W_qkv, b_qkv, sin_tab, cos_tab, out_0, out_1, out_2):
    nc = tc.nc
    outs = (out_0, out_1, out_2)
    with ExitStack() as ctx:
        ctx.enter_context(tc.manual_schedule())
        keep = ctx.enter_context(tc.tile_pool(name="keep", bufs=1))
        x_grouped_pool = ctx.enter_context(tc.tile_pool(name="x_grouped", bufs=2))
        w_grouped_pool = ctx.enter_context(tc.tile_pool(name="w_grouped", bufs=3))
        products_pool = ctx.enter_context(tc.tile_pool(name="products", bufs=4))
        unit_out_pool = ctx.enter_context(tc.tile_pool(name="unit_out", bufs=5))
        turned_bias_pool = ctx.enter_context(tc.tile_pool(name="turned_bias", bufs=3))
        v_T_pool = ctx.enter_context(tc.tile_pool(name="v_T", bufs=4))
        v_out_pool = ctx.enter_context(tc.tile_pool(name="v_out", bufs=2))
        psum = ctx.enter_context(tc.psum_pool(name="psum", bufs=8))

        x_raw = [keep.tile([P, B, E], BF16, name="x_raw%d" % j) for j in range(TILES)]
        w_raw = [keep.tile([P, 4 * PASSES, BANK], BF16, name="w_raw%d" % c) for c in range(len(CHUNKS))]
        w_codes = [keep.tile([P, PASSES, BANK], U32, name="w_codes%d" % c, align_bytes=64) for c in range(len(CHUNKS))]
        w_scales = [keep.tile([P, PASSES, BANK], U8, name="w_scales%d" % c, align_bytes=64) for c in range(len(CHUNKS))]
        x_codes = keep.tile([P, B, PASSES, TILES, P], U32, align_bytes=64)
        x_scales = keep.tile([P, B, PASSES, TILES, P], U8, align_bytes=64)
        cos16 = keep.tile([P, TILES, R], BF16)
        sin16 = keep.tile([P, TILES, R], BF16)
        factors = keep.tile([P, TILES, 2, R], F32)
        table = keep.tile([P, TILES, P], BF16)
        table_T = keep.tile([P, TILES, P], BF16)
        bias_rows = keep.tile([P, P], BF16)
        bias_masked = keep.tile([P, 2 * H, R], BF16)
        mask = keep.tile([P, R], F32)
        selector = keep.tile([P, P], BF16)
        pass_bias = keep.tile([P, 2 * H, R], F32)
        v_bias = keep.tile([P, 2 * FEATURE_TILES], F32)
        ident = keep.tile([P, P], F32)
        ident16 = keep.tile([P, P], BF16)

        nc.vector.memset(bias_rows[:], 0.0)
        nc.vector.memset(table[:], 0.0)
        nc.vector.memset(selector[:], 0.0)
        nc.vector.memset(selector[2 * R:3 * R, :], 1.0)
        make_identity(nc, ident[:])

        def load_x(j):
            nc.sync.dma_start(out=x_raw[j][:], in_=x[:, j * P:(j + 1) * P, :].rearrange("b p k -> p b k"))

        def load_w(c, passes):
            c0 = CHUNKS[c][0] * E + CHUNKS[c][1] * BANK
            for g in passes:
                for u in range(2):
                    r0 = 4 * P * g + 2 * P * u
                    nc.sync.dma_start(
                        out=w_raw[c][:, 4 * g + 2 * u:4 * g + 2 * u + 2, :],
                        in_=W_qkv[r0:r0 + 2 * P, c0:c0 + BANK].rearrange("(q e) c -> q e c", e=2),
                    )

        nc.sync.dma_start(out=cos16[:], in_=cos_tab.rearrange("(t p) j -> p t j", p=P))
        nc.sync.dma_start(out=sin16[:], in_=sin_tab.rearrange("(t p) j -> p t j", p=P))
        qk_bias = b_qkv[0:2 * E].rearrange("(r d) -> r d", d=D)
        nc.sync.dma_start(out=bias_rows[0:2 * H, 0:R], in_=qk_bias[:, 0:R])
        nc.sync.dma_start(out=bias_rows[0:2 * H, R:2 * R], in_=qk_bias[:, 0:R])
        nc.sync.dma_start(out=bias_rows[0:2 * H, 2 * R:3 * R], in_=qk_bias[:, R:D])
        nc.sync.dma_start(
            out=bias_rows[2 * H:2 * H + 2 * FEATURE_TILES, :], in_=b_qkv[2 * E:3 * E].rearrange("(r c) -> r c", c=P)
        )
        load_w(0, (0,))
        load_x(0)
        load_w(0, (1,))
        load_x(1)
        load_w(4, range(PASSES))
        load_x(2)
        load_x(3)
        for c in (1, 2, 5, 3):
            load_w(c, range(PASSES))

        nc.vector.tensor_copy(out=ident16[:], in_=ident[:])
        nc.vector.tensor_tensor(out=mask[:], in0=ident[:, 0:R], in1=ident[:, 2 * R:3 * R], op=ALU.add)
        nc.vector.tensor_tensor(
            out=mask[:, 0:HALF], in0=mask[:, 0:HALF], in1=ident[:, R + HALF:2 * R], op=ALU.add
        )
        nc.vector.tensor_tensor(out=mask[:, HALF:R], in0=mask[:, HALF:R], in1=ident[:, R:R + HALF], op=ALU.add)
        nc.vector.tensor_copy(out=factors[:, :, 0, :], in_=cos16[:])
        nc.vector.tensor_copy(out=factors[:, :, 1, 0:HALF], in_=sin16[:, :, HALF:R])
        nc.vector.tensor_scalar_mul(out=factors[:, :, 1, HALF:R], in0=sin16[:, :, 0:HALF], scalar1=-1.0)
        nc.vector.tensor_copy(out=table[:, :, 0:2 * R], in_=factors[:].rearrange("p t c j -> p t (c j)"))

        def mx_product(out, lhsT, lhsT_scale, rhs, rhs_scale):
            for g in range(PASSES):
                nc.tensor.matmul_mx(
                    out=out,
                    lhsT=lhsT(g).bitcast(FP8X4),
                    lhsT_scale=lhsT_scale(g),
                    rhs=rhs(g).bitcast(FP8X4),
                    rhs_scale=rhs_scale(g),
                    start=(g == 0),
                    stop=(g == PASSES - 1),
                )

        def transpose_x(j):
            grouped = x_grouped_pool.tile([P, B, PASSES, P, 4], BF16, name="x_grouped", tag="x_grouped", align_bytes=64)
            banks = []
            for b in range(B):
                words = x_raw[j][:, b, :].bitcast(F32)
                bank = psum.tile([P, 2 * PASSES, P], F32, name="x_bank", tag="bank")
                for gu in range(2 * PASSES):
                    nc.tensor.transpose(bank[:, gu, :], words[:, gu * P:(gu + 1) * P], ident[:])
                banks.append(bank)
            for b in range(B):
                nc.scalar.copy(
                    out=grouped[:].bitcast(F32)[:, b], in_=banks[b][:].rearrange("p (g u) r -> p g r u", u=2)
                )
            return grouped

        def quantise_x(j, grouped):
            for b in range(B):
                for g in range(PASSES):
                    nc.vector.quantize_mx(
                        out=x_codes[:, b, g, j, :].bitcast(FP8X4),
                        scales=x_scales[:, b, g, j, :],
                        in_=grouped[:, b, g].rearrange("p r t -> p (r t)"),
                    )

        w_grouped = {}

        def regroup_w(copy, pieces, c, g):
            if g == 0:
                w_grouped[c] = w_grouped_pool.tile(
                    [P, PASSES, BANK, 4], BF16, name="w_grouped", tag="w_grouped", align_bytes=64
                )
            width = BANK // pieces
            for i in range(pieces):
                copy(
                    out=w_grouped[c][:, g, i * width:(i + 1) * width, :].rearrange("p (c i) t -> p c t i", i=4),
                    in_=w_raw[c][:, 4 * g:4 * g + 4, i * width:(i + 1) * width].rearrange("p t (c i) -> p c t i", i=4),
                )

        def quantise_w(c):
            nc.vector.quantize_mx(
                out=w_codes[c][:].rearrange("p g c -> p (g c)").bitcast(FP8X4),
                scales=w_scales[c][:].rearrange("p g c -> p (g c)"),
                in_=w_grouped[c][:].rearrange("p g c t -> p (g c t)"),
            )

        def unit_products(unit):
            c, j = unit // TILES, unit % TILES
            head0 = CHUNKS[c][0] * H + CHUNKS[c][1] * HEADS
            turned_bank = psum.tile([P, HEADS, R], F32, name="turned_bank", tag="bank")
            nc.tensor.matmul(
                out=turned_bank[:].rearrange("p h j -> p (h j)"),
                lhsT=table_T[:, j, :],
                rhs=bias_masked[:, head0:head0 + HEADS, :].rearrange("p r j -> p (r j)"),
                start=True,
                stop=True,
            )
            banks = []
            for b in range(B):
                bank = psum.tile([P, BANK], F32, name="unit_bank", tag="bank")
                mx_product(
                    bank[:],
                    lambda g: x_codes[:, b, g, j, :],
                    lambda g: x_scales[:, b, g, j, :],
                    lambda g: w_codes[c][:, g, :],
                    lambda g: w_scales[c][:, g, :],
                )
                banks.append(bank)
            turned_bias = turned_bank
            if not vector_adds_turned_bias(unit):
                turned_bias = turned_bias_pool.tile([P, HEADS, R], F32, name="turned_bias", tag="turned_bias")
                nc.scalar.copy(out=turned_bias[:], in_=turned_bank[:])
            return banks, turned_bias

        def unit_finish(unit, banks, turned_bias):
            c, j = unit // TILES, unit % TILES
            which, half = CHUNKS[c]
            head0 = which * H + half * HEADS
            products = products_pool.tile([P, B, HEADS, 2, R], F32, name="products", tag="products")
            result = unit_out_pool.tile([P, B, BANK], F32, name="unit_out", tag="unit_out")
            for b in range(B):
                heads = banks[b][:].rearrange("p (h d) -> p h d", d=D)
                nc.vector.tensor_tensor(
                    out=products[:, b],
                    in0=heads[:, :, 0:R].unsqueeze(2).to_broadcast([P, HEADS, 2, R]),
                    in1=factors[:, j].unsqueeze(1).to_broadcast([P, HEADS, 2, R]),
                    op=ALU.mult,
                )
                nc.vector.tensor_tensor(
                    out=result[:, b, :].rearrange("p (h d) -> p h d", d=D)[:, :, R:D],
                    in0=heads[:, :, R:D],
                    in1=pass_bias[:, head0:head0 + HEADS, :],
                    op=ALU.add,
                )
            for_both = turned_bias[:].unsqueeze(1).to_broadcast([P, B, HEADS, R])
            if vector_adds_turned_bias(unit):
                with_cos = products[:, :, :, 0, :]
                nc.vector.tensor_tensor(out=with_cos, in0=with_cos, in1=for_both, op=ALU.add)
            heads = result[:].rearrange("p b (h d) -> p (b h) d", d=D)
            pairs = products[:].rearrange("p b h c j -> p (b h) c j")
            nc.gpsimd.tensor_tensor(
                out=heads[:, :, 0:HALF], in0=pairs[:, :, 0, 0:HALF], in1=pairs[:, :, 1, HALF:R], op=ALU.add
            )
            nc.gpsimd.tensor_tensor(
                out=heads[:, :, HALF:R], in0=pairs[:, :, 0, HALF:R], in1=pairs[:, :, 1, 0:HALF], op=ALU.add
            )
            if not vector_adds_turned_bias(unit):
                turned = result[:].rearrange("p b (h d) -> p b h d", d=D)[:, :, :, 0:R]
                nc.gpsimd.tensor_tensor(out=turned, in0=turned, in1=for_both, op=ALU.add)
            dst = outs[which].rearrange("b s h d -> s b (h d)")
            nc.sync.dma_start(out=dst[j * P:(j + 1) * P, :, half * BANK:(half + 1) * BANK], in_=result[:])

        v_T = {}
        v_out = {}

        def v_front(pair):
            banks = []
            for n in (2 * pair, 2 * pair + 1):
                c, b, f = V_CHUNKS[n // STEPS_PER_CHUNK], (n // FEATURE_TILES) % B, n % FEATURE_TILES
                bank = psum.tile([P, BANK], F32, name="v_bank", tag="bank")
                mx_product(
                    bank[:],
                    lambda g: w_codes[c][:, g, f * P:(f + 1) * P],
                    lambda g: w_scales[c][:, g, f * P:(f + 1) * P],
                    lambda g: x_codes[:, b, g].rearrange("p j r -> p (j r)"),
                    lambda g: x_scales[:, b, g].rearrange("p j r -> p (j r)"),
                )
                banks.append(bank)
            for n in (2 * pair, 2 * pair + 1):
                column = CHUNKS[V_CHUNKS[n // STEPS_PER_CHUNK]][1] * FEATURE_TILES + n % FEATURE_TILES
                v_T[n] = v_T_pool.tile([P, BANK], F32, name="v_T", tag="v_T")
                nc.scalar.activation(
                    out=v_T[n][:], in_=banks[n % 2][:], func=ACT.Identity, bias=v_bias[:, column:column + 1], scale=1.0
                )

        def v_back(pair):
            banks = []
            for n in (2 * pair, 2 * pair + 1):
                bank = psum.tile([P, TILES, P], F32, name="v_back", tag="bank")
                for j in range(TILES):
                    nc.tensor.transpose(bank[:, j, :], v_T[n][:, j * P:(j + 1) * P], ident[:])
                banks.append(bank)
            for n in (2 * pair, 2 * pair + 1):
                quarter, f = n // FEATURE_TILES, n % FEATURE_TILES
                if f == 0:
                    v_out[quarter] = v_out_pool.tile([P, TILES, BANK], F32, name="v_out", tag="v_out")
                nc.scalar.copy(out=v_out[quarter][:, :, f * P:(f + 1) * P], in_=banks[n % 2][:])
                if f == FEATURE_TILES - 1:
                    half, b = CHUNKS[V_CHUNKS[quarter // B]][1], quarter % B
                    dst = out_2.rearrange("b (j p) h d -> p b j (h d)", p=P)
                    nc.sync.dma_start(out=dst[:, b, :, half * BANK:(half + 1) * BANK], in_=v_out[quarter][:])

        table_bank = psum.tile([P, TILES, P], BF16, name="table_bank", tag="bank")
        for t in range(TILES):
            nc.tensor.transpose(table_bank[:, t, :], table[:, t, :], ident16[:])
        bias_bank = psum.tile([P, P], BF16, name="bias_bank", tag="bank")
        nc.tensor.transpose(bias_bank[:], bias_rows[:], ident16[:])
        nc.scalar.copy(out=table_T[:], in_=table_bank[:])
        nc.vector.tensor_tensor(
            out=bias_masked[:],
            in0=bias_bank[:, 0:2 * H].unsqueeze(2).to_broadcast([P, 2 * H, R]),
            in1=mask[:].unsqueeze(1).to_broadcast([P, 2 * H, R]),
            op=ALU.mult,
        )
        nc.vector.tensor_copy(out=v_bias[:], in_=bias_bank[:, 2 * H:2 * H + 2 * FEATURE_TILES])
        x_grouped = {0: transpose_x(0)}
        pass_banks = []
        for w in range(2):
            pass_bank = psum.tile([P, H, R], F32, name="pass_bank", tag="bank")
            nc.tensor.matmul(
                out=pass_bank[:].rearrange("p h j -> p (h j)"),
                lhsT=selector[:],
                rhs=bias_masked[:, w * H:(w + 1) * H, :].rearrange("p r j -> p (r j)"),
                start=True,
                stop=True,
            )
            pass_banks.append(pass_bank)
        for w in range(2):
            nc.scalar.copy(out=pass_bias[:, w * H:(w + 1) * H, :], in_=pass_banks[w][:])
        for g in range(PASSES):
            regroup_w(nc.vector.tensor_copy, 1, 0, g)
        quantise_x(0, x_grouped[0])
        quantise_w(0)
        x_grouped[1] = transpose_x(1)
        quantise_x(1, x_grouped[1])

        scalar_passes = [(c, g) for c in (4, 1, 2, 5, 3) for g in range(PASSES)]
        v_parts = []
        for pair in range(V_PAIRS + 1):
            if pair < V_PAIRS:
                v_parts.append(("front", pair))
            if pair >= 1:
                v_parts.append(("back", pair - 1))
        quantise_after = {3: (4, 1), 6: (2,), 8: (5,), 10: (3,)}
        placed = 0
        for unit in range(UNITS):
            banks, turned_bias = unit_products(unit)
            if unit == 1:
                for j in (2, 3):
                    x_grouped[j] = transpose_x(j)
            for i in range((1, 1, 2, 2)[unit] if unit < 4 else 0):
                regroup_w(nc.scalar.copy, 2, scalar_passes[0][0], scalar_passes[0][1])
                scalar_passes = scalar_passes[1:]
            while placed < min(len(v_parts), (3 * (unit - 4) + 1) // 2):
                part, pair = v_parts[placed]
                if part == "front":
                    v_front(pair)
                else:
                    v_back(pair)
                if scalar_passes and placed % 2 == 0:
                    regroup_w(nc.scalar.copy, 2, scalar_passes[0][0], scalar_passes[0][1])
                    scalar_passes = scalar_passes[1:]
                placed += 1
            unit_finish(unit, banks, turned_bias)
            if unit == 1:
                for j in (2, 3):
                    quantise_x(j, x_grouped[j])
            for c in quantise_after.get(unit, ()):
                quantise_w(c)
